import numpy as np
import ml_dtypes


def mxq(x, axis, fmt="e4m3"):
    dtype, down = {"e4m3": (ml_dtypes.float8_e4m3fn, 7), "e5m2": (ml_dtypes.float8_e5m2, 14)}[fmt]
    v = np.moveaxis(np.asarray(x, np.float32).astype(ml_dtypes.bfloat16).astype(np.float64), axis, -1)
    blocks = v.reshape(v.shape[:-1] + (-1, 32))
    amax = np.abs(blocks).max(-1, keepdims=True)
    byte = np.maximum(np.where(amax > 0, np.frexp(amax)[1] - 1 + 127, 0) - down, 1)
    scale = np.exp2(byte - 127.0)
    codes = (blocks / scale).astype(np.float32).astype(dtype).astype(np.float64)
    return np.moveaxis((codes * scale).reshape(v.shape), -1, axis)


WIDE = False


def mx_kscale(k):
    if not WIDE:
        return np.ones(k)
    levels = np.array([10, -10, 5, -5, 0])
    if k % 512:
        return np.exp2(np.random.permutation(np.resize(levels, k // 32))).repeat(32)
    a = np.empty((k // 512, 16))
    for p in range(k // 512):
        a[p, :8] = np.random.permutation(np.resize(levels, 8))
        for g in range(8):
            far = levels[np.abs(levels - a[p, g]) >= 10]
            a[p, g + 8] = far[np.random.randint(len(far))]
    return np.exp2(a.ravel()).repeat(32)


BF16 = ml_dtypes.bfloat16


def bf(x):
    return np.asarray(x, np.float32).astype(BF16)


def f64(x):
    return np.asarray(x).astype(np.float64)


B, C, HH, WW, NH, HD, F = 4, 512, 16, 16, 8, 64, 2048
E = NH * HD


def setup_inputs():
    s, t = mx_kscale(E), mx_kscale(C)
    return {"o": bf(np.random.standard_normal((B, HH, WW, E)) * 0.6 * s),
            "xn": bf(np.random.standard_normal((B, HH, WW, C)) * 0.5 * t),
            "W_O": bf(np.random.standard_normal((E, C)) / np.sqrt(E) / s[:, None] * t),
            "scale_attn": bf(0.5 * (1.0 + 0.1 * np.random.standard_normal(1))),
            "ffn1_w": bf(np.random.standard_normal((F, C)) * 3.0 / np.sqrt(C) / t),
            "ffn1_b": bf(np.random.standard_normal(F) * 0.3),
            "scale_ffn": bf(0.1 * (1.0 + 0.1 * np.random.standard_normal(1)))}


def reference(o, xn, W_O, scale_attn, ffn1_w, ffn1_b, scale_ffn):
    p = (mxq(f64(o), 3, "e4m3") @ mxq(f64(W_O), 0, "e4m3")) * f64(scale_attn)
    y = np.maximum(f64(xn) + p, 0.0)
    u = (mxq(y, 3, "e4m3") @ mxq(f64(ffn1_w), 1, "e4m3").T) + f64(ffn1_b)
    return np.maximum(u * f64(scale_ffn), 0.0)

@@ -1,0 +1,295 @@
+from contextlib import ExitStack
+
+import concourse.masks as masks
+import concourse.mybir as mybir
+
+F32 = mybir.dt.float32
+BF16 = mybir.dt.bfloat16
+U32 = mybir.dt.uint32
+U8 = mybir.dt.uint8
+FP8X4 = mybir.dt.float8_e4m3fn_x4
+ALU = mybir.AluOpType
+ACT = mybir.ActivationFunctionType
+
+P = 128
+PACK = 4
+TOKENS = 4 * 16 * 16
+K = 512
+F = 2048
+TILES = TOKENS // P
+HALF = TILES // 2
+CHUNK = 512
+CHUNKS = F // CHUNK
+ROWS = CHUNK // P
+PAIRS = TILES // 2
+ROUND = 2 * CHUNKS
+BANKS = PAIRS * ROUND
+W_BANKS = 2 * CHUNKS
+AHEAD = 2
+
+FLOPS = 2 * TOKENS * K * K + 2 * TOKENS * K * F
+
+
+def tile_transformerconvblock_pb_kernel(
+    tc, o, xn, W_O, scale_attn, ffn1_w, ffn1_b, scale_ffn, out
+):
+    nc = tc.nc
+    with ExitStack() as ctx:
+        keep = ctx.enter_context(tc.tile_pool(name="keep", bufs=1))
+        results = ctx.enter_context(tc.tile_pool(name="results", bufs=12))
+        psum_words = ctx.enter_context(tc.psum_pool(name="psum_words", bufs=2))
+        psum_first = ctx.enter_context(tc.psum_pool(name="psum_first", bufs=3))
+        psum_u = ctx.enter_context(tc.psum_pool(name="psum_u", bufs=AHEAD + 1))
+
+        o_dram = o.rearrange("b h w e -> (b h w) e").rearrange("(p i) e -> p i e", i=TILES)
+        xn_dram = xn.rearrange("b h w c -> (b h w) c").rearrange("(p i) c -> p i c", i=TILES)
+        out_dram = out.rearrange("b h w f -> (b h w) f").rearrange("(p i) f -> p i f", i=TILES)
+        w_dram = ffn1_w.rearrange("(n j r) c -> j n r c", n=CHUNKS, r=ROWS)
+        wo_dram = W_O.rearrange("(q t) c -> q t c", t=PACK)
+
+        bias_row = keep.tile([P, F], BF16)
+        attn_bf16 = keep.tile([P, 1], BF16)
+        ffn_bf16 = keep.tile([P, 1], BF16)
+        attn = keep.tile([P, 1], F32)
+        ffn = keep.tile([P, 1], F32)
+        ident_f32 = keep.tile([P, P], F32)
+        ident_bf16 = keep.tile([P, P], BF16)
+        ones = keep.tile([P, P], BF16)
+        wo_raw = keep.tile([P, PACK * K], BF16)
+        o_sb = keep.tile([P, TILES * K], BF16)
+        xn_sb = keep.tile([P, TILES * K], BF16)
+        w_sb = keep.tile([P, CHUNKS * ROWS * K], BF16)
+        o_tiles = o_sb[:].rearrange("p (i e) -> p i e", i=TILES)
+        xn_tiles = xn_sb[:].rearrange("p (i c) -> p i c", i=TILES)
+        w_chunks = w_sb[:].rearrange("j (n r c) -> j n r c", n=CHUNKS, r=ROWS)
+        first = slice(0, HALF)
+        second = slice(HALF, TILES)
+
+        wo_grouped = keep.tile([P, K * PACK], BF16, align_bytes=64)
+        wo_codes = keep.tile([P, K], U32, align_bytes=64)
+        wo_scales = keep.tile([P, K], U8, align_bytes=64)
+        o_grouped = keep.tile([P, TOKENS * PACK], BF16, align_bytes=64)
+        o_codes = keep.tile([P, TOKENS], U32, align_bytes=64)
+        o_scales = keep.tile([P, TOKENS], U8, align_bytes=64)
+        w_grouped = keep.tile([P, F * PACK], BF16, align_bytes=64)
+        w_codes = keep.tile([P, F], U32, align_bytes=64)
+        w_scales = keep.tile([P, F], U8, align_bytes=64)
+        y_grouped = keep.tile([P, TOKENS * PACK], BF16, align_bytes=64)
+        y_codes = keep.tile([P, TOKENS], U32, align_bytes=64)
+        y_scales = keep.tile([P, TOKENS], U8, align_bytes=64)
+        z_sb = keep.tile([P, TILES * K], BF16)
+        bias_all = keep.tile([P, F], BF16)
+
+        def quantise(grouped, codes, scales, start, count):
+            nc.vector.quantize_mx(
+                out=codes[:, start : start + count].bitcast(FP8X4),
+                scales=scales[:, start : start + count],
+                in_=grouped[:, PACK * start : PACK * (start + count)],
+            )
+
+        o_words = o_sb[:].bitcast(F32).rearrange("p (i q u) -> p i q u", i=TILES, u=2)
+        o_grouped_words = o_grouped[:].bitcast(F32).rearrange("q (i p u) -> q i p u", i=TILES, u=2)
+        w_words = w_sb[:].bitcast(F32).rearrange(
+            "j (n r q u) -> j n r q u", n=CHUNKS, r=ROWS, u=2
+        )
+        w_grouped_words = w_grouped[:].bitcast(F32).rearrange(
+            "q (n j r u) -> q n j r u", n=CHUNKS, r=ROWS, u=2
+        )
+
+        def transpose_o(pair):
+            i = 2 * pair
+            bank = psum_words.tile([P, 2, 2, P], F32, tag="words")
+            for a in range(2):
+                for u in range(2):
+                    nc.tensor.transpose(bank[:, a, u, :], o_words[:, i + a, :, u], ident_f32[:])
+            nc.scalar.copy(
+                out=o_grouped_words[:, i : i + 2, :, :],
+                in_=bank[:].rearrange("q a u p -> q a p u"),
+            )
+
+        def transpose_w(k):
+            n, r = k // 2, 2 * (k % 2)
+            bank = psum_words.tile([P, 2, 2, P], F32, tag="words")
+            for a in range(2):
+                for u in range(2):
+                    nc.tensor.transpose(bank[:, a, u, :], w_words[:, n, r + a, :, u], ident_f32[:])
+            copy = nc.vector.tensor_copy if n == 0 else nc.scalar.copy
+            copy(
+                out=w_grouped_words[:, n, :, r : r + 2, :],
+                in_=bank[:].rearrange("q a u j -> q j a u"),
+            )
+
+        def spread_bias(half):
+            b = half * 2 * CHUNK
+            bank = psum_u.tile([P, 2 * CHUNK], BF16, tag="u")
+            for c in range(0, 2 * CHUNK, CHUNK):
+                nc.tensor.matmul(
+                    out=bank[:, c : c + CHUNK],
+                    lhsT=ones[:],
+                    rhs=bias_row[:, b + c : b + c + CHUNK],
+                    start=True,
+                    stop=True,
+                )
+            nc.scalar.copy(out=bias_all[:, b : b + 2 * CHUNK], in_=bank[:])
+
+        z_words = z_sb[:].rearrange("p (i q t) -> p i q t", i=TILES, t=PACK)
+        y_grouped_tiles = y_grouped[:].rearrange("q (i p t) -> q i p t", i=TILES, t=PACK)
+        p_banks = {}
+        z_banks = {}
+        u_banks = {}
+
+        def first_matmul(i):
+            tokens = slice(i * P, (i + 1) * P)
+            p_banks[i] = psum_first.tile([P, K], F32, name="p_bank", tag="first")
+            nc.tensor.matmul_mx(
+                out=p_banks[i][:],
+                lhsT=o_codes[:, tokens].bitcast(FP8X4),
+                lhsT_scale=o_scales[:, tokens],
+                rhs=wo_codes[:].bitcast(FP8X4),
+                rhs_scale=wo_scales[:],
+                start=True,
+                stop=True,
+            )
+
+        def add_xn(i):
+            cols = slice(i * K, (i + 1) * K)
+            nc.vector.scalar_tensor_tensor(
+                out=z_sb[:, cols],
+                in0=p_banks[i][:],
+                scalar=attn[:, 0:1],
+                in1=xn_sb[:, cols],
+                op0=ALU.mult,
+                op1=ALU.add,
+            )
+
+        def transpose_z(i):
+            z_banks[i] = psum_first.tile([P, PACK, P], BF16, name="z_bank", tag="first")
+            for t in range(PACK):
+                nc.tensor.transpose(z_banks[i][:, t, :], z_words[:, i, :, t], ident_bf16[:])
+
+        def relu_z(i):
+            nc.scalar.activation(
+                out=y_grouped_tiles[:, i, :, :],
+                in_=z_banks[i][:].rearrange("q t p -> q p t"),
+                func=ACT.Relu,
+            )
+
+        def tile_and_chunk(b):
+            pair, rest = divmod(b, ROUND)
+            return 2 * pair + rest % 2, rest // 2
+
+        def second_matmul(b):
+            j, n = tile_and_chunk(b)
+            tokens = slice(j * P, (j + 1) * P)
+            cols = slice(n * CHUNK, (n + 1) * CHUNK)
+            u_banks[b] = psum_u.tile([P, CHUNK], F32, name="u_bank", tag="u")
+            nc.tensor.matmul_mx(
+                out=u_banks[b][:],
+                lhsT=y_codes[:, tokens].bitcast(FP8X4),
+                lhsT_scale=y_scales[:, tokens],
+                rhs=w_codes[:, cols].bitcast(FP8X4),
+                rhs_scale=w_scales[:, cols],
+                start=True,
+                stop=True,
+            )
+
+        def second_epilogue(b):
+            j, n = tile_and_chunk(b)
+            cols = slice(n * CHUNK, (n + 1) * CHUNK)
+            h_tile = results.tile([P, CHUNK], F32, tag="h")
+            nc.vector.tensor_tensor(out=h_tile[:], in0=u_banks[b][:], in1=bias_all[:, cols], op=ALU.add)
+            nc.scalar.activation(out=h_tile[:], in_=h_tile[:], func=ACT.Relu, scale=ffn[:, 0:1])
+            nc.sync.dma_start(out=out_dram[:, j, cols], in_=h_tile[:])
+
+        def quantise_o(pair):
+            quantise(o_grouped, o_codes, o_scales, 2 * pair * P, 2 * P)
+
+        def quantise_y(pair):
+            quantise(y_grouped, y_codes, y_scales, 2 * pair * P, 2 * P)
+
+        def quantise_w(n):
+            quantise(w_grouped, w_codes, w_scales, n * CHUNK, CHUNK)
+
+        def load_everything():
+            nc.vector.memset(bias_row[:], 0.0)
+            nc.scalar.dma_start(out=bias_row[0:1, :], in_=ffn1_b.rearrange("(a f) -> a f", a=1))
+            with nc.allow_non_contiguous_dma(reason="one bfloat16 scalar to every partition"):
+                nc.scalar.dma_start(out=attn_bf16[:], in_=scale_attn.partition_broadcast(P))
+                nc.scalar.dma_start(out=ffn_bf16[:], in_=scale_ffn.partition_broadcast(P))
+            nc.sync.dma_start(out=wo_raw[:].rearrange("q (t c) -> q t c", t=PACK), in_=wo_dram)
+            nc.sync.dma_start(out=o_tiles[:, first, :], in_=o_dram[:, first, :])
+            nc.sync.dma_start(out=xn_tiles[:, first, :], in_=xn_dram[:, first, :])
+            for n in range(CHUNKS):
+                nc.sync.dma_start(out=w_chunks[:, n], in_=w_dram[:, n])
+            nc.sync.dma_start(out=o_tiles[:, second, :], in_=o_dram[:, second, :])
+            nc.sync.dma_start(out=xn_tiles[:, second, :], in_=xn_dram[:, second, :])
+
+        def make_constants():
+            nc.vector.memset(ident_f32[:], 0.0)
+            masks.make_identity(nc, ident_f32[:], nomemset=True)
+            nc.vector.tensor_copy(out=ident_bf16[:], in_=ident_f32[:])
+            nc.vector.memset(ones[:], 1.0)
+            nc.gpsimd.tensor_copy(out=attn[:], in_=attn_bf16[:])
+            nc.gpsimd.tensor_copy(out=ffn[:], in_=ffn_bf16[:])
+
+        with tc.manual_schedule():
+            load_everything()
+            make_constants()
+            nc.vector.tensor_copy(
+                out=wo_grouped[:].rearrange("q (c t) -> q c t", t=PACK),
+                in_=wo_raw[:].rearrange("q (t c) -> q c t", t=PACK),
+            )
+            quantise(wo_grouped, wo_codes, wo_scales, 0, K)
+            transpose_o(0)
+            quantise_o(0)
+            transpose_o(1)
+            spread_bias(0)
+            first_matmul(0)
+            first_matmul(1)
+            add_xn(0)
+            add_xn(1)
+            transpose_w(0)
+            transpose_w(1)
+            transpose_z(0)
+            transpose_z(1)
+            relu_z(0)
+            relu_z(1)
+            quantise_o(1)
+            quantise_w(0)
+            transpose_w(2)
+            transpose_w(3)
+            quantise_y(0)
+            spread_bias(1)
+
+        for s in range(BANKS + AHEAD):
+            this_pair, t = divmod(s, ROUND)
+            pair = this_pair + 1
+            a = 2 * pair
+            if s < BANKS:
+                second_matmul(s)
+            if s + 4 < W_BANKS:
+                transpose_w(s + 4)
+            if pair + 1 < PAIRS and t == 4:
+                transpose_o(pair + 1)
+            if pair < PAIRS and t == 0:
+                first_matmul(a)
+                first_matmul(a + 1)
+            if pair < PAIRS and t == 2:
+                transpose_z(a)
+            if pair < PAIRS and t == 3:
+                transpose_z(a + 1)
+                relu_z(a)
+            if pair < PAIRS and t == 4:
+                relu_z(a + 1)
+            if s >= AHEAD:
+                second_epilogue(s - AHEAD)
+            if s % 2 == 0 and s // 2 + 1 < CHUNKS:
+                quantise_w(s // 2 + 1)
+            if pair < PAIRS and t == 1:
+                add_xn(a)
+            if pair < PAIRS and t == 2:
+                add_xn(a + 1)
+            if pair < PAIRS and t == 7:
+                quantise_y(pair)
+            if pair + 1 < PAIRS and t == 7:
+                quantise_o(pair + 1)

@@ -17,15 +17,14 @@ TOKENS = 4 * 16 * 16
 K = 512
 F = 2048
 TILES = TOKENS // P
-HALF = TILES // 2
 CHUNK = 512
 CHUNKS = F // CHUNK
 ROWS = CHUNK // P
 PAIRS = TILES // 2
 ROUND = 2 * CHUNKS
 BANKS = PAIRS * ROUND
-W_BANKS = 2 * CHUNKS
-AHEAD = 2
+AHEAD = 3
+WO_SPLIT = 88
 
 FLOPS = 2 * TOKENS * K * K + 2 * TOKENS * K * F
 
@@ -38,7 +37,7 @@ def tile_transformerconvblock_pb_kernel(
         keep = ctx.enter_context(tc.tile_pool(name="keep", bufs=1))
         results = ctx.enter_context(tc.tile_pool(name="results", bufs=12))
         psum_words = ctx.enter_context(tc.psum_pool(name="psum_words", bufs=2))
-        psum_first = ctx.enter_context(tc.psum_pool(name="psum_first", bufs=3))
+        psum_first = ctx.enter_context(tc.psum_pool(name="psum_first", bufs=2))
         psum_u = ctx.enter_context(tc.psum_pool(name="psum_u", bufs=AHEAD + 1))
 
         o_dram = o.rearrange("b h w e -> (b h w) e").rearrange("(p i) e -> p i e", i=TILES)
@@ -52,8 +51,8 @@ def tile_transformerconvblock_pb_kernel(
         ffn_bf16 = keep.tile([P, 1], BF16)
         attn = keep.tile([P, 1], F32)
         ffn = keep.tile([P, 1], F32)
+        warm = keep.tile([P, 1], F32)
         ident_f32 = keep.tile([P, P], F32)
-        ident_bf16 = keep.tile([P, P], BF16)
         ones = keep.tile([P, P], BF16)
         wo_raw = keep.tile([P, PACK * K], BF16)
         o_sb = keep.tile([P, TILES * K], BF16)
@@ -62,8 +61,6 @@ def tile_transformerconvblock_pb_kernel(
         o_tiles = o_sb[:].rearrange("p (i e) -> p i e", i=TILES)
         xn_tiles = xn_sb[:].rearrange("p (i c) -> p i c", i=TILES)
         w_chunks = w_sb[:].rearrange("j (n r c) -> j n r c", n=CHUNKS, r=ROWS)
-        first = slice(0, HALF)
-        second = slice(HALF, TILES)
 
         wo_grouped = keep.tile([P, K * PACK], BF16, align_bytes=64)
         wo_codes = keep.tile([P, K], U32, align_bytes=64)
@@ -77,7 +74,7 @@ def tile_transformerconvblock_pb_kernel(
         y_grouped = keep.tile([P, TOKENS * PACK], BF16, align_bytes=64)
         y_codes = keep.tile([P, TOKENS], U32, align_bytes=64)
         y_scales = keep.tile([P, TOKENS], U8, align_bytes=64)
-        z_sb = keep.tile([P, TILES * K], BF16)
+        xn_grouped = keep.tile([P, TOKENS * PACK], BF16, align_bytes=64)
         bias_all = keep.tile([P, F], BF16)
 
         def quantise(grouped, codes, scales, start, count):
@@ -87,8 +84,11 @@ def tile_transformerconvblock_pb_kernel(
                 in_=grouped[:, PACK * start : PACK * (start + count)],
             )
 
-        o_words = o_sb[:].bitcast(F32).rearrange("p (i q u) -> p i q u", i=TILES, u=2)
+        token_words = "p (i q u) -> p i q u"
+        o_words = o_sb[:].bitcast(F32).rearrange(token_words, i=TILES, u=2)
+        xn_words = xn_sb[:].bitcast(F32).rearrange(token_words, i=TILES, u=2)
         o_grouped_words = o_grouped[:].bitcast(F32).rearrange("q (i p u) -> q i p u", i=TILES, u=2)
+        xn_grouped_words = xn_grouped[:].bitcast(F32).rearrange("q (i p u) -> q i p u", i=TILES, u=2)
         w_words = w_sb[:].bitcast(F32).rearrange(
             "j (n r q u) -> j n r q u", n=CHUNKS, r=ROWS, u=2
         )
@@ -96,32 +96,37 @@ def tile_transformerconvblock_pb_kernel(
             "q (n j r u) -> q n j r u", n=CHUNKS, r=ROWS, u=2
         )
 
-        def transpose_o(pair):
+        def transpose_tokens(words, grouped_words, pair):
             i = 2 * pair
-            bank = psum_words.tile([P, 2, 2, P], F32, tag="words")
+            bank = psum_words.tile([P, 2, 2, P], F32, name="bank", tag="words")
             for a in range(2):
                 for u in range(2):
-                    nc.tensor.transpose(bank[:, a, u, :], o_words[:, i + a, :, u], ident_f32[:])
+                    nc.tensor.transpose(bank[:, a, u, :], words[:, i + a, :, u], ident_f32[:])
             nc.scalar.copy(
-                out=o_grouped_words[:, i : i + 2, :, :],
+                out=grouped_words[:, i : i + 2, :, :],
                 in_=bank[:].rearrange("q a u p -> q a p u"),
             )
 
+        def transpose_o(pair):
+            transpose_tokens(o_words, o_grouped_words, pair)
+
+        def transpose_xn(pair):
+            transpose_tokens(xn_words, xn_grouped_words, pair)
+
         def transpose_w(k):
             n, r = k // 2, 2 * (k % 2)
-            bank = psum_words.tile([P, 2, 2, P], F32, tag="words")
+            bank = psum_words.tile([P, 2, 2, P], F32, name="bank", tag="words")
             for a in range(2):
                 for u in range(2):
                     nc.tensor.transpose(bank[:, a, u, :], w_words[:, n, r + a, :, u], ident_f32[:])
-            copy = nc.vector.tensor_copy if n == 0 else nc.scalar.copy
-            copy(
+            nc.scalar.copy(
                 out=w_grouped_words[:, n, :, r : r + 2, :],
                 in_=bank[:].rearrange("q a u j -> q j a u"),
             )
 
         def spread_bias(half):
             b = half * 2 * CHUNK
-            bank = psum_u.tile([P, 2 * CHUNK], BF16, tag="u")
+            bank = psum_u.tile([P, 2 * CHUNK], BF16, name="bias_bank", tag="u")
             for c in range(0, 2 * CHUNK, CHUNK):
                 nc.tensor.matmul(
                     out=bank[:, c : c + CHUNK],
@@ -132,47 +137,38 @@ def tile_transformerconvblock_pb_kernel(
                 )
             nc.scalar.copy(out=bias_all[:, b : b + 2 * CHUNK], in_=bank[:])
 
-        z_words = z_sb[:].rearrange("p (i q t) -> p i q t", i=TILES, t=PACK)
-        y_grouped_tiles = y_grouped[:].rearrange("q (i p t) -> q i p t", i=TILES, t=PACK)
         p_banks = {}
-        z_banks = {}
         u_banks = {}
 
         def first_matmul(i):
             tokens = slice(i * P, (i + 1) * P)
-            p_banks[i] = psum_first.tile([P, K], F32, name="p_bank", tag="first")
-            nc.tensor.matmul_mx(
-                out=p_banks[i][:],
-                lhsT=o_codes[:, tokens].bitcast(FP8X4),
-                lhsT_scale=o_scales[:, tokens],
-                rhs=wo_codes[:].bitcast(FP8X4),
-                rhs_scale=wo_scales[:],
-                start=True,
-                stop=True,
-            )
+            p_banks[i] = psum_first.tile([P, PACK, P], F32, name="p_bank", tag="first")
+            for t in range(PACK):
+                channels = slice(t * P, (t + 1) * P)
+                nc.tensor.matmul_mx(
+                    out=p_banks[i][:, t, :],
+                    lhsT=wo_codes[:, channels].bitcast(FP8X4),
+                    lhsT_scale=wo_scales[:, channels],
+                    rhs=o_codes[:, tokens].bitcast(FP8X4),
+                    rhs_scale=o_scales[:, tokens],
+                    start=True,
+                    stop=True,
+                )
 
         def add_xn(i):
             cols = slice(i * K, (i + 1) * K)
             nc.vector.scalar_tensor_tensor(
-                out=z_sb[:, cols],
-                in0=p_banks[i][:],
+                out=y_grouped[:, cols].rearrange("q (p t) -> q p t", t=PACK),
+                in0=p_banks[i][:].rearrange("q t p -> q p t"),
                 scalar=attn[:, 0:1],
-                in1=xn_sb[:, cols],
+                in1=xn_grouped[:, cols].rearrange("q (p t) -> q p t", t=PACK),
                 op0=ALU.mult,
                 op1=ALU.add,
             )
 
-        def transpose_z(i):
-            z_banks[i] = psum_first.tile([P, PACK, P], BF16, name="z_bank", tag="first")
-            for t in range(PACK):
-                nc.tensor.transpose(z_banks[i][:, t, :], z_words[:, i, :, t], ident_bf16[:])
-
-        def relu_z(i):
-            nc.scalar.activation(
-                out=y_grouped_tiles[:, i, :, :],
-                in_=z_banks[i][:].rearrange("q t p -> q p t"),
-                func=ACT.Relu,
-            )
+        def relu_y(i):
+            cols = slice(i * K, (i + 1) * K)
+            nc.vector.tensor_scalar_max(y_grouped[:, cols], y_grouped[:, cols], 0.0)
 
         def tile_and_chunk(b):
             pair, rest = divmod(b, ROUND)
@@ -196,7 +192,7 @@ def tile_transformerconvblock_pb_kernel(
         def second_epilogue(b):
             j, n = tile_and_chunk(b)
             cols = slice(n * CHUNK, (n + 1) * CHUNK)
-            h_tile = results.tile([P, CHUNK], F32, tag="h")
+            h_tile = results.tile([P, CHUNK], F32, name="h_tile", tag="h")
             nc.vector.tensor_tensor(out=h_tile[:], in0=u_banks[b][:], in1=bias_all[:, cols], op=ALU.add)
             nc.scalar.activation(out=h_tile[:], in_=h_tile[:], func=ACT.Relu, scale=ffn[:, 0:1])
             nc.sync.dma_start(out=out_dram[:, j, cols], in_=h_tile[:])
@@ -204,61 +200,68 @@ def tile_transformerconvblock_pb_kernel(
         def quantise_o(pair):
             quantise(o_grouped, o_codes, o_scales, 2 * pair * P, 2 * P)
 
-        def quantise_y(pair):
-            quantise(y_grouped, y_codes, y_scales, 2 * pair * P, 2 * P)
+        def quantise_y(i):
+            quantise(y_grouped, y_codes, y_scales, i * P, P)
 
         def quantise_w(n):
             quantise(w_grouped, w_codes, w_scales, n * CHUNK, CHUNK)
 
+        def load_tokens(first, last):
+            tiles = slice(first, last)
+            nc.sync.dma_start(out=o_tiles[:, tiles, :], in_=o_dram[:, tiles, :])
+            nc.sync.dma_start(out=xn_tiles[:, tiles, :], in_=xn_dram[:, tiles, :])
+
         def load_everything():
-            nc.vector.memset(bias_row[:], 0.0)
-            nc.scalar.dma_start(out=bias_row[0:1, :], in_=ffn1_b.rearrange("(a f) -> a f", a=1))
+            nc.sync.dma_start(out=wo_raw[:].rearrange("q (t c) -> q t c", t=PACK), in_=wo_dram)
+            load_tokens(0, 2)
+            nc.sync.dma_start(out=w_chunks[:, 0], in_=w_dram[:, 0])
+            nc.sync.dma_start(out=w_chunks[:, 1], in_=w_dram[:, 1])
+            load_tokens(2, 4)
+            nc.sync.dma_start(out=w_chunks[:, 2], in_=w_dram[:, 2])
+            nc.sync.dma_start(out=w_chunks[:, 3], in_=w_dram[:, 3])
+            load_tokens(4, 8)
             with nc.allow_non_contiguous_dma(reason="one bfloat16 scalar to every partition"):
                 nc.scalar.dma_start(out=attn_bf16[:], in_=scale_attn.partition_broadcast(P))
                 nc.scalar.dma_start(out=ffn_bf16[:], in_=scale_ffn.partition_broadcast(P))
-            nc.sync.dma_start(out=wo_raw[:].rearrange("q (t c) -> q t c", t=PACK), in_=wo_dram)
-            nc.sync.dma_start(out=o_tiles[:, first, :], in_=o_dram[:, first, :])
-            nc.sync.dma_start(out=xn_tiles[:, first, :], in_=xn_dram[:, first, :])
-            for n in range(CHUNKS):
-                nc.sync.dma_start(out=w_chunks[:, n], in_=w_dram[:, n])
-            nc.sync.dma_start(out=o_tiles[:, second, :], in_=o_dram[:, second, :])
-            nc.sync.dma_start(out=xn_tiles[:, second, :], in_=xn_dram[:, second, :])
 
         def make_constants():
             nc.vector.memset(ident_f32[:], 0.0)
-            masks.make_identity(nc, ident_f32[:], nomemset=True)
-            nc.vector.tensor_copy(out=ident_bf16[:], in_=ident_f32[:])
+            nc.vector.memset(warm[:], 0.0)
             nc.vector.memset(ones[:], 1.0)
+            masks.make_identity(nc, ident_f32[:], nomemset=True)
+            nc.gpsimd.memset(bias_row[:].bitcast(U32), 0)
+            nc.gpsimd.dma_start(out=bias_row[0:1, :], in_=ffn1_b.rearrange("(a f) -> a f", a=1))
+            nc.scalar.activation(out=warm[:], in_=warm[:], func=ACT.Relu)
             nc.gpsimd.tensor_copy(out=attn[:], in_=attn_bf16[:])
             nc.gpsimd.tensor_copy(out=ffn[:], in_=ffn_bf16[:])
+
+        wo_to = wo_grouped[:].rearrange("q (t m r) -> q t m r", t=PACK, r=PACK)
+        wo_from = wo_raw[:].rearrange("q (r m t) -> q t m r", t=PACK, r=PACK)
 
         with tc.manual_schedule():
             load_everything()
             make_constants()
-            nc.vector.tensor_copy(
-                out=wo_grouped[:].rearrange("q (c t) -> q c t", t=PACK),
-                in_=wo_raw[:].rearrange("q (t c) -> q c t", t=PACK),
-            )
+            nc.vector.tensor_copy(out=wo_to[:, :, :WO_SPLIT, :], in_=wo_from[:, :, :WO_SPLIT, :])
+            nc.scalar.copy(out=wo_to[:, :, WO_SPLIT:, :], in_=wo_from[:, :, WO_SPLIT:, :])
             quantise(wo_grouped, wo_codes, wo_scales, 0, K)
             transpose_o(0)
             quantise_o(0)
-            transpose_o(1)
-            spread_bias(0)
+            transpose_xn(0)
+            transpose_w(0)
             first_matmul(0)
             first_matmul(1)
+            transpose_w(1)
             add_xn(0)
             add_xn(1)
-            transpose_w(0)
-            transpose_w(1)
-            transpose_z(0)
-            transpose_z(1)
-            relu_z(0)
-            relu_z(1)
-            quantise_o(1)
+            spread_bias(0)
             quantise_w(0)
+            relu_y(0)
+            relu_y(1)
             transpose_w(2)
-            transpose_w(3)
             quantise_y(0)
+            quantise_y(1)
+            transpose_w(3)
+            transpose_o(1)
             spread_bias(1)
 
         for s in range(BANKS + AHEAD):
@@ -267,29 +270,31 @@ def tile_transformerconvblock_pb_kernel(
             a = 2 * pair
             if s < BANKS:
                 second_matmul(s)
-            if s + 4 < W_BANKS:
+            if s == 0:
+                quantise_w(1)
+                quantise_o(1)
+            if s < 4:
                 transpose_w(s + 4)
-            if pair + 1 < PAIRS and t == 4:
-                transpose_o(pair + 1)
-            if pair < PAIRS and t == 0:
-                first_matmul(a)
-                first_matmul(a + 1)
-            if pair < PAIRS and t == 2:
-                transpose_z(a)
-            if pair < PAIRS and t == 3:
-                transpose_z(a + 1)
-                relu_z(a)
-            if pair < PAIRS and t == 4:
-                relu_z(a + 1)
-            if s >= AHEAD:
-                second_epilogue(s - AHEAD)
-            if s % 2 == 0 and s // 2 + 1 < CHUNKS:
+            if s in (2, 4):
                 quantise_w(s // 2 + 1)
             if pair < PAIRS and t == 1:
-                add_xn(a)
+                transpose_xn(pair)
             if pair < PAIRS and t == 2:
+                first_matmul(a)
+                first_matmul(a + 1)
+            if pair + 1 < PAIRS and t == 5:
+                transpose_o(pair + 1)
+            if s >= AHEAD:
+                second_epilogue(s - AHEAD)
+            if pair < PAIRS and t == 3:
+                add_xn(a)
+            if pair < PAIRS and t == 4:
                 add_xn(a + 1)
-            if pair < PAIRS and t == 7:
-                quantise_y(pair)
+                relu_y(a)
+            if pair < PAIRS and t == 5:
+                relu_y(a + 1)
+                quantise_y(a)
+            if pair < PAIRS and t == 6:
+                quantise_y(a + 1)
             if pair + 1 < PAIRS and t == 7:
                 quantise_o(pair + 1)

@@ -21,10 +21,10 @@ CHUNK = 512
 CHUNKS = F // CHUNK
 ROWS = CHUNK // P
 PAIRS = TILES // 2
-ROUND = 2 * CHUNKS
-BANKS = PAIRS * ROUND
-AHEAD = 3
-WO_SPLIT = 88
+ROUND = 4 * CHUNKS
+BANKS = PAIRS // 2 * ROUND
+AHEAD = 2
+WO_SPLIT = 104
 
 FLOPS = 2 * TOKENS * K * K + 2 * TOKENS * K * F
 
@@ -36,7 +36,7 @@ def tile_transformerconvblock_pb_kernel(
     with ExitStack() as ctx:
         keep = ctx.enter_context(tc.tile_pool(name="keep", bufs=1))
         results = ctx.enter_context(tc.tile_pool(name="results", bufs=12))
-        psum_words = ctx.enter_context(tc.psum_pool(name="psum_words", bufs=2))
+        psum_words = ctx.enter_context(tc.psum_pool(name="psum_words", bufs=3))
         psum_first = ctx.enter_context(tc.psum_pool(name="psum_first", bufs=2))
         psum_u = ctx.enter_context(tc.psum_pool(name="psum_u", bufs=AHEAD + 1))
 
@@ -46,14 +46,15 @@ def tile_transformerconvblock_pb_kernel(
         w_dram = ffn1_w.rearrange("(n j r) c -> j n r c", n=CHUNKS, r=ROWS)
         wo_dram = W_O.rearrange("(q t) c -> q t c", t=PACK)
 
-        bias_row = keep.tile([P, F], BF16)
+        bias_rows = keep.tile([P, CHUNK], BF16)
         attn_bf16 = keep.tile([P, 1], BF16)
         ffn_bf16 = keep.tile([P, 1], BF16)
         attn = keep.tile([P, 1], F32)
         ffn = keep.tile([P, 1], F32)
         warm = keep.tile([P, 1], F32)
         ident_f32 = keep.tile([P, P], F32)
-        ones = keep.tile([P, P], BF16)
+        ident_bf16 = keep.tile([P, P], BF16)
+        zeros = keep.tile([P, CHUNK], BF16)
         wo_raw = keep.tile([P, PACK * K], BF16)
         o_sb = keep.tile([P, TILES * K], BF16)
         xn_sb = keep.tile([P, TILES * K], BF16)
@@ -124,21 +125,27 @@ def tile_transformerconvblock_pb_kernel(
                 in_=bank[:].rearrange("q a u j -> q j a u"),
             )
 
-        def spread_bias(half):
+        def spread_bias(half, copy):
             b = half * 2 * CHUNK
             bank = psum_u.tile([P, 2 * CHUNK], BF16, name="bias_bank", tag="u")
-            for c in range(0, 2 * CHUNK, CHUNK):
+            for c in range(2):
+                n = 2 * half + c
                 nc.tensor.matmul(
-                    out=bank[:, c : c + CHUNK],
-                    lhsT=ones[:],
-                    rhs=bias_row[:, b + c : b + c + CHUNK],
+                    out=bank[:, c * CHUNK : (c + 1) * CHUNK],
+                    lhsT=ident_bf16[:, n : n + 1].to_broadcast([P, P]),
+                    rhs=bias_rows[:],
                     start=True,
                     stop=True,
                 )
-            nc.scalar.copy(out=bias_all[:, b : b + 2 * CHUNK], in_=bank[:])
+            copy(out=bias_all[:, b : b + 2 * CHUNK], in_=bank[:])
 
         p_banks = {}
         u_banks = {}
+
+        def warm_up(count):
+            bank = psum_u.tile([P, CHUNK], F32, name="idle_bank", tag="u")
+            for c in range(count):
+                nc.tensor.matmul(out=bank[:], lhsT=zeros[:, :P], rhs=zeros[:], start=True, stop=True)
 
         def first_matmul(i):
             tokens = slice(i * P, (i + 1) * P)
@@ -171,8 +178,10 @@ def tile_transformerconvblock_pb_kernel(
             nc.vector.tensor_scalar_max(y_grouped[:, cols], y_grouped[:, cols], 0.0)
 
         def tile_and_chunk(b):
-            pair, rest = divmod(b, ROUND)
-            return 2 * pair + rest % 2, rest // 2
+            fours, rest = divmod(b, ROUND)
+            half, rest = divmod(rest, ROUND // 2)
+            pair, rest = divmod(rest, 4)
+            return 4 * fours + 2 * pair + rest % 2, 2 * half + rest // 2
 
         def second_matmul(b):
             j, n = tile_and_chunk(b)
@@ -206,95 +215,113 @@ def tile_transformerconvblock_pb_kernel(
         def quantise_w(n):
             quantise(w_grouped, w_codes, w_scales, n * CHUNK, CHUNK)
 
-        def load_tokens(first, last):
-            tiles = slice(first, last)
-            nc.sync.dma_start(out=o_tiles[:, tiles, :], in_=o_dram[:, tiles, :])
-            nc.sync.dma_start(out=xn_tiles[:, tiles, :], in_=xn_dram[:, tiles, :])
+        def load(tiles, dram, first, last):
+            rows = slice(first, last)
+            nc.sync.dma_start(out=tiles[:, rows, :], in_=dram[:, rows, :])
 
         def load_everything():
-            nc.sync.dma_start(out=wo_raw[:].rearrange("q (t c) -> q t c", t=PACK), in_=wo_dram)
-            load_tokens(0, 2)
-            nc.sync.dma_start(out=w_chunks[:, 0], in_=w_dram[:, 0])
-            nc.sync.dma_start(out=w_chunks[:, 1], in_=w_dram[:, 1])
-            load_tokens(2, 4)
-            nc.sync.dma_start(out=w_chunks[:, 2], in_=w_dram[:, 2])
-            nc.sync.dma_start(out=w_chunks[:, 3], in_=w_dram[:, 3])
-            load_tokens(4, 8)
             with nc.allow_non_contiguous_dma(reason="one bfloat16 scalar to every partition"):
                 nc.scalar.dma_start(out=attn_bf16[:], in_=scale_attn.partition_broadcast(P))
                 nc.scalar.dma_start(out=ffn_bf16[:], in_=scale_ffn.partition_broadcast(P))
+            nc.vector.memset(bias_rows[:], 0.0)
+            load(o_tiles, o_dram, 0, 2)
+            nc.sync.dma_start(out=wo_raw[:].rearrange("q (t c) -> q t c", t=PACK), in_=wo_dram)
+            nc.sync.dma_start(out=bias_rows[0:CHUNKS, :], in_=ffn1_b.rearrange("(n f) -> n f", n=CHUNKS))
+            load(xn_tiles, xn_dram, 0, 2)
+            nc.sync.dma_start(out=w_chunks[:, 0], in_=w_dram[:, 0])
+            nc.sync.dma_start(out=w_chunks[:, 1], in_=w_dram[:, 1])
+            load(o_tiles, o_dram, 2, 4)
+            load(xn_tiles, xn_dram, 2, 4)
+            nc.sync.dma_start(out=w_chunks[:, 2], in_=w_dram[:, 2])
+            nc.sync.dma_start(out=w_chunks[:, 3], in_=w_dram[:, 3])
+            load(o_tiles, o_dram, 4, 8)
+            load(xn_tiles, xn_dram, 4, 8)
 
         def make_constants():
-            nc.vector.memset(ident_f32[:], 0.0)
-            nc.vector.memset(warm[:], 0.0)
-            nc.vector.memset(ones[:], 1.0)
+            nc.gpsimd.memset(ident_f32[:], 0.0)
+            nc.gpsimd.memset(zeros[:], 0.0)
             masks.make_identity(nc, ident_f32[:], nomemset=True)
-            nc.gpsimd.memset(bias_row[:].bitcast(U32), 0)
-            nc.gpsimd.dma_start(out=bias_row[0:1, :], in_=ffn1_b.rearrange("(a f) -> a f", a=1))
+            nc.vector.memset(warm[:], 0.0)
             nc.scalar.activation(out=warm[:], in_=warm[:], func=ACT.Relu)
+            nc.vector.tensor_copy(out=ident_bf16[:], in_=ident_f32[:])
             nc.gpsimd.tensor_copy(out=attn[:], in_=attn_bf16[:])
             nc.gpsimd.tensor_copy(out=ffn[:], in_=ffn_bf16[:])
 
         wo_to = wo_grouped[:].rearrange("q (t m r) -> q t m r", t=PACK, r=PACK)
         wo_from = wo_raw[:].rearrange("q (r m t) -> q t m r", t=PACK, r=PACK)
 
-        with tc.manual_schedule():
-            load_everything()
-            make_constants()
-            nc.vector.tensor_copy(out=wo_to[:, :, :WO_SPLIT, :], in_=wo_from[:, :, :WO_SPLIT, :])
-            nc.scalar.copy(out=wo_to[:, :, WO_SPLIT:, :], in_=wo_from[:, :, WO_SPLIT:, :])
-            quantise(wo_grouped, wo_codes, wo_scales, 0, K)
-            transpose_o(0)
-            quantise_o(0)
-            transpose_xn(0)
-            transpose_w(0)
-            first_matmul(0)
-            first_matmul(1)
-            transpose_w(1)
-            add_xn(0)
-            add_xn(1)
-            spread_bias(0)
-            quantise_w(0)
-            relu_y(0)
-            relu_y(1)
-            transpose_w(2)
-            quantise_y(0)
-            quantise_y(1)
-            transpose_w(3)
-            transpose_o(1)
-            spread_bias(1)
+        ctx.enter_context(tc.manual_schedule())
+        load_everything()
+        make_constants()
 
-        for s in range(BANKS + AHEAD):
-            this_pair, t = divmod(s, ROUND)
-            pair = this_pair + 1
-            a = 2 * pair
-            if s < BANKS:
-                second_matmul(s)
+        warm_up(4)
+        transpose_o(0)
+        nc.vector.tensor_copy(out=wo_to[:, :, :WO_SPLIT, :], in_=wo_from[:, :, :WO_SPLIT, :])
+        nc.scalar.copy(out=wo_to[:, :, WO_SPLIT:, :], in_=wo_from[:, :, WO_SPLIT:, :])
+        quantise_o(0)
+        quantise(wo_grouped, wo_codes, wo_scales, 0, K)
+        spread_bias(0, nc.vector.tensor_copy)
+        transpose_xn(0)
+        transpose_w(0)
+        first_matmul(0)
+        transpose_w(1)
+        first_matmul(1)
+        add_xn(0)
+        relu_y(0)
+        quantise_y(0)
+        transpose_w(2)
+        transpose_w(3)
+        quantise_w(0)
+        second_matmul(0)
+        add_xn(1)
+        relu_y(1)
+        transpose_o(1)
+        quantise_y(1)
+        second_matmul(1)
+        transpose_xn(1)
+
+        for s in range(BANKS):
+            if s in (1, 2):
+                transpose_w(s + 3)
+            if s == 3:
+                spread_bias(1, nc.scalar.copy)
+            if s in (4, 5):
+                transpose_w(s + 2)
+            if s in (6, 9):
+                transpose_o(s // 3)
+            if s in (7, 10):
+                transpose_xn(s // 3)
+            second_epilogue(s)
             if s == 0:
-                quantise_w(1)
                 quantise_o(1)
-            if s < 4:
-                transpose_w(s + 4)
-            if s in (2, 4):
-                quantise_w(s // 2 + 1)
-            if pair < PAIRS and t == 1:
-                transpose_xn(pair)
-            if pair < PAIRS and t == 2:
-                first_matmul(a)
-                first_matmul(a + 1)
-            if pair + 1 < PAIRS and t == 5:
-                transpose_o(pair + 1)
-            if s >= AHEAD:
-                second_epilogue(s - AHEAD)
-            if pair < PAIRS and t == 3:
-                add_xn(a)
-            if pair < PAIRS and t == 4:
-                add_xn(a + 1)
-                relu_y(a)
-            if pair < PAIRS and t == 5:
-                relu_y(a + 1)
-                quantise_y(a)
-            if pair < PAIRS and t == 6:
-                quantise_y(a + 1)
-            if pair + 1 < PAIRS and t == 7:
-                quantise_o(pair + 1)
+                first_matmul(2)
+                first_matmul(3)
+                quantise_w(1)
+            if s == 1:
+                add_xn(2)
+                add_xn(3)
+            if s == 2:
+                relu_y(2)
+                relu_y(3)
+                quantise_y(2)
+                quantise_y(3)
+            if s in (4, 6):
+                quantise_w(s // 2)
+            for pair, first in ((2, 8), (3, 13)):
+                a = 2 * pair
+                if s == first:
+                    quantise_o(pair)
+                    first_matmul(a)
+                    first_matmul(a + 1)
+                if s == first + 1:
+                    add_xn(a)
+                if s == first + 2:
+                    add_xn(a + 1)
+                if s == first + 3:
+                    relu_y(a)
+                    relu_y(a + 1)
+                if s == first + 4:
+                    quantise_y(a)
+                    quantise_y(a + 1)
+            if s + AHEAD < BANKS:
+                second_matmul(s + AHEAD)

@@ -23,6 +23,7 @@ ROWS = CHUNK // P
 PAIRS = TILES // 2
 ROUND = 4 * CHUNKS
 BANKS = PAIRS // 2 * ROUND
+LAG = 2
 AHEAD = 2
 WO_SPLIT = 104
 
@@ -35,7 +36,7 @@ def tile_transformerconvblock_pb_kernel(
     nc = tc.nc
     with ExitStack() as ctx:
         keep = ctx.enter_context(tc.tile_pool(name="keep", bufs=1))
-        results = ctx.enter_context(tc.tile_pool(name="results", bufs=12))
+        results = ctx.enter_context(tc.tile_pool(name="results", bufs=16))
         psum_words = ctx.enter_context(tc.psum_pool(name="psum_words", bufs=3))
         psum_first = ctx.enter_context(tc.psum_pool(name="psum_first", bufs=2))
         psum_u = ctx.enter_context(tc.psum_pool(name="psum_u", bufs=AHEAD + 1))
@@ -97,9 +98,16 @@ def tile_transformerconvblock_pb_kernel(
             "q (n j r u) -> q n j r u", n=CHUNKS, r=ROWS, u=2
         )
 
+        def fill(bank):
+            nc.tensor.matmul(
+                out=bank[:].rearrange("q a u p -> q (a u p)"), lhsT=zeros[:, :P], rhs=zeros[:], start=True, stop=True
+            )
+
         def transpose_tokens(words, grouped_words, pair):
             i = 2 * pair
             bank = psum_words.tile([P, 2, 2, P], F32, name="bank", tag="words")
+            if pair == 1:
+                fill(bank)
             for a in range(2):
                 for u in range(2):
                     nc.tensor.transpose(bank[:, a, u, :], words[:, i + a, :, u], ident_f32[:])
@@ -117,6 +125,8 @@ def tile_transformerconvblock_pb_kernel(
         def transpose_w(k):
             n, r = k // 2, 2 * (k % 2)
             bank = psum_words.tile([P, 2, 2, P], F32, name="bank", tag="words")
+            if k in (0, 1, 2, 4, 5):
+                fill(bank)
             for a in range(2):
                 for u in range(2):
                     nc.tensor.transpose(bank[:, a, u, :], w_words[:, n, r + a, :, u], ident_f32[:])
@@ -198,13 +208,20 @@ def tile_transformerconvblock_pb_kernel(
                 stop=True,
             )
 
-        def second_epilogue(b):
+        h_tiles = {}
+
+        def add_bias(b):
             j, n = tile_and_chunk(b)
             cols = slice(n * CHUNK, (n + 1) * CHUNK)
-            h_tile = results.tile([P, CHUNK], F32, name="h_tile", tag="h")
-            nc.vector.tensor_tensor(out=h_tile[:], in0=u_banks[b][:], in1=bias_all[:, cols], op=ALU.add)
-            nc.scalar.activation(out=h_tile[:], in_=h_tile[:], func=ACT.Relu, scale=ffn[:, 0:1])
-            nc.sync.dma_start(out=out_dram[:, j, cols], in_=h_tile[:])
+            h_tiles[b] = results.tile([P, CHUNK], F32, name="h_tile", tag="h")
+            nc.vector.tensor_tensor(out=h_tiles[b][:], in0=u_banks[b][:], in1=bias_all[:, cols], op=ALU.add)
+
+        def relu_h(b):
+            j, n = tile_and_chunk(b)
+            cols = slice(n * CHUNK, (n + 1) * CHUNK)
+            h = h_tiles[b][:]
+            nc.scalar.activation(out=h, in_=h, func=ACT.Relu, scale=ffn[:, 0:1])
+            nc.sync.dma_start(out=out_dram[:, j, cols], in_=h)
 
         def quantise_o(pair):
             quantise(o_grouped, o_codes, o_scales, 2 * pair * P, 2 * P)
@@ -220,26 +237,24 @@ def tile_transformerconvblock_pb_kernel(
             nc.sync.dma_start(out=tiles[:, rows, :], in_=dram[:, rows, :])
 
         def load_everything():
-            with nc.allow_non_contiguous_dma(reason="one bfloat16 scalar to every partition"):
-                nc.scalar.dma_start(out=attn_bf16[:], in_=scale_attn.partition_broadcast(P))
-                nc.scalar.dma_start(out=ffn_bf16[:], in_=scale_ffn.partition_broadcast(P))
+            nc.vector.memset(zeros[:], 0.0)
             nc.vector.memset(bias_rows[:], 0.0)
             load(o_tiles, o_dram, 0, 2)
             nc.sync.dma_start(out=wo_raw[:].rearrange("q (t c) -> q t c", t=PACK), in_=wo_dram)
             nc.sync.dma_start(out=bias_rows[0:CHUNKS, :], in_=ffn1_b.rearrange("(n f) -> n f", n=CHUNKS))
             load(xn_tiles, xn_dram, 0, 2)
             nc.sync.dma_start(out=w_chunks[:, 0], in_=w_dram[:, 0])
+            with nc.allow_non_contiguous_dma(reason="one bfloat16 scalar to every partition"):
+                nc.sync.dma_start(out=attn_bf16[:], in_=scale_attn.partition_broadcast(P))
+                nc.sync.dma_start(out=ffn_bf16[:], in_=scale_ffn.partition_broadcast(P))
             nc.sync.dma_start(out=w_chunks[:, 1], in_=w_dram[:, 1])
-            load(o_tiles, o_dram, 2, 4)
-            load(xn_tiles, xn_dram, 2, 4)
+            load(o_tiles, o_dram, 2, TILES)
+            load(xn_tiles, xn_dram, 2, TILES)
             nc.sync.dma_start(out=w_chunks[:, 2], in_=w_dram[:, 2])
             nc.sync.dma_start(out=w_chunks[:, 3], in_=w_dram[:, 3])
-            load(o_tiles, o_dram, 4, 8)
-            load(xn_tiles, xn_dram, 4, 8)
 
         def make_constants():
             nc.gpsimd.memset(ident_f32[:], 0.0)
-            nc.gpsimd.memset(zeros[:], 0.0)
             masks.make_identity(nc, ident_f32[:], nomemset=True)
             nc.vector.memset(warm[:], 0.0)
             nc.scalar.activation(out=warm[:], in_=warm[:], func=ACT.Relu)
@@ -254,7 +269,7 @@ def tile_transformerconvblock_pb_kernel(
         load_everything()
         make_constants()
 
-        warm_up(4)
+        warm_up(3)
         transpose_o(0)
         nc.vector.tensor_copy(out=wo_to[:, :, :WO_SPLIT, :], in_=wo_from[:, :, :WO_SPLIT, :])
         nc.scalar.copy(out=wo_to[:, :, WO_SPLIT:, :], in_=wo_from[:, :, WO_SPLIT:, :])
@@ -276,27 +291,28 @@ def tile_transformerconvblock_pb_kernel(
         add_xn(1)
         relu_y(1)
         transpose_o(1)
+        transpose_xn(1)
+        quantise_w(1)
         quantise_y(1)
         second_matmul(1)
-        transpose_xn(1)
 
-        for s in range(BANKS):
-            if s in (1, 2):
-                transpose_w(s + 3)
-            if s == 3:
+        for s in range(BANKS + LAG):
+            if s in (0, 1, 3, 4):
+                transpose_w(s + 4 if s < 2 else s + 3)
+            if s == 2:
                 spread_bias(1, nc.scalar.copy)
-            if s in (4, 5):
-                transpose_w(s + 2)
             if s in (6, 9):
                 transpose_o(s // 3)
             if s in (7, 10):
                 transpose_xn(s // 3)
-            second_epilogue(s)
+            if s < BANKS:
+                add_bias(s)
+            if s >= LAG:
+                relu_h(s - LAG)
             if s == 0:
                 quantise_o(1)
                 first_matmul(2)
                 first_matmul(3)
-                quantise_w(1)
             if s == 1:
                 add_xn(2)
                 add_xn(3)

@@ -23,7 +23,7 @@ ROWS = CHUNK // P
 PAIRS = TILES // 2
 ROUND = 4 * CHUNKS
 BANKS = PAIRS // 2 * ROUND
-LAG = 2
+LAG = 3
 AHEAD = 2
 WO_SPLIT = 104
 
@@ -36,7 +36,7 @@ def tile_transformerconvblock_pb_kernel(
     nc = tc.nc
     with ExitStack() as ctx:
         keep = ctx.enter_context(tc.tile_pool(name="keep", bufs=1))
-        results = ctx.enter_context(tc.tile_pool(name="results", bufs=16))
+        results = ctx.enter_context(tc.tile_pool(name="results", bufs=10))
         psum_words = ctx.enter_context(tc.psum_pool(name="psum_words", bufs=3))
         psum_first = ctx.enter_context(tc.psum_pool(name="psum_first", bufs=2))
         psum_u = ctx.enter_context(tc.psum_pool(name="psum_u", bufs=AHEAD + 1))
@@ -190,8 +190,8 @@ def tile_transformerconvblock_pb_kernel(
         def tile_and_chunk(b):
             fours, rest = divmod(b, ROUND)
             half, rest = divmod(rest, ROUND // 2)
-            pair, rest = divmod(rest, 4)
-            return 4 * fours + 2 * pair + rest % 2, 2 * half + rest // 2
+            tile, chunk = divmod(rest, 2)
+            return 4 * fours + tile, 2 * half + chunk
 
         def second_matmul(b):
             j, n = tile_and_chunk(b)
@@ -213,15 +213,25 @@ def tile_transformerconvblock_pb_kernel(
         def add_bias(b):
             j, n = tile_and_chunk(b)
             cols = slice(n * CHUNK, (n + 1) * CHUNK)
-            h_tiles[b] = results.tile([P, CHUNK], F32, name="h_tile", tag="h")
-            nc.vector.tensor_tensor(out=h_tiles[b][:], in0=u_banks[b][:], in1=bias_all[:, cols], op=ALU.add)
+            if b % 2 == 0:
+                h_tiles[b // 2] = results.tile([P, 2 * CHUNK], F32, name="h_tile", tag="h")
+            nc.vector.tensor_tensor(
+                out=h_tiles[b // 2][:, b % 2 * CHUNK : (b % 2 + 1) * CHUNK],
+                in0=u_banks[b][:],
+                in1=bias_all[:, cols],
+                op=ALU.add,
+            )
 
-        def relu_h(b):
-            j, n = tile_and_chunk(b)
-            cols = slice(n * CHUNK, (n + 1) * CHUNK)
-            h = h_tiles[b][:]
-            nc.scalar.activation(out=h, in_=h, func=ACT.Relu, scale=ffn[:, 0:1])
-            nc.sync.dma_start(out=out_dram[:, j, cols], in_=h)
+        def relu_h(d):
+            j, n = tile_and_chunk(2 * d)
+            h = h_tiles[d][:]
+            pieces = 2 if d == BANKS // 2 - 1 else 1
+            width = 2 * CHUNK // pieces
+            for c in range(0, 2 * CHUNK, width):
+                part = h[:, c : c + width]
+                first = n * CHUNK + c
+                nc.scalar.activation(out=part, in_=part, func=ACT.Relu, scale=ffn[:, 0:1])
+                nc.sync.dma_start(out=out_dram[:, j, first : first + width], in_=part)
 
         def quantise_o(pair):
             quantise(o_grouped, o_codes, o_scales, 2 * pair * P, 2 * P)
@@ -288,12 +298,11 @@ def tile_transformerconvblock_pb_kernel(
         transpose_w(3)
         quantise_w(0)
         second_matmul(0)
-        add_xn(1)
-        relu_y(1)
         transpose_o(1)
         transpose_xn(1)
+        add_xn(1)
         quantise_w(1)
-        quantise_y(1)
+        relu_y(1)
         second_matmul(1)
 
         for s in range(BANKS + LAG):
@@ -307,19 +316,22 @@ def tile_transformerconvblock_pb_kernel(
                 transpose_xn(s // 3)
             if s < BANKS:
                 add_bias(s)
-            if s >= LAG:
-                relu_h(s - LAG)
+            if s >= LAG and (s - LAG) % 2 == 0:
+                relu_h((s - LAG) // 2)
             if s == 0:
+                quantise_y(1)
                 quantise_o(1)
                 first_matmul(2)
                 first_matmul(3)
             if s == 1:
                 add_xn(2)
-                add_xn(3)
             if s == 2:
                 relu_y(2)
-                relu_y(3)
                 quantise_y(2)
+                add_xn(3)
+            if s == 3:
+                relu_y(3)
+            if s == 4:
                 quantise_y(3)
             if s in (4, 6):
                 quantise_w(s // 2)
@@ -329,14 +341,14 @@ def tile_transformerconvblock_pb_kernel(
                     quantise_o(pair)
                     first_matmul(a)
                     first_matmul(a + 1)
-                if s == first + 1:
-                    add_xn(a)
                 if s == first + 2:
-                    add_xn(a + 1)
+                    add_xn(a)
                 if s == first + 3:
+                    add_xn(a + 1)
+                if s == first + 4:
                     relu_y(a)
                     relu_y(a + 1)
-                if s == first + 4:
+                if s == first + 5:
                     quantise_y(a)
                     quantise_y(a + 1)
             if s + AHEAD < BANKS:

@@ -23,8 +23,8 @@ ROWS = CHUNK // P
 PAIRS = TILES // 2
 ROUND = 4 * CHUNKS
 BANKS = PAIRS // 2 * ROUND
-LAG = 3
-AHEAD = 2
+LAG = 4
+AHEAD = 3
 WO_SPLIT = 104
 
 FLOPS = 2 * TOKENS * K * K + 2 * TOKENS * K * F
@@ -37,9 +37,7 @@ def tile_transformerconvblock_pb_kernel(
     with ExitStack() as ctx:
         keep = ctx.enter_context(tc.tile_pool(name="keep", bufs=1))
         results = ctx.enter_context(tc.tile_pool(name="results", bufs=10))
-        psum_words = ctx.enter_context(tc.psum_pool(name="psum_words", bufs=3))
-        psum_first = ctx.enter_context(tc.psum_pool(name="psum_first", bufs=2))
-        psum_u = ctx.enter_context(tc.psum_pool(name="psum_u", bufs=AHEAD + 1))
+        psum = ctx.enter_context(tc.psum_pool(name="psum", bufs=8))
 
         o_dram = o.rearrange("b h w e -> (b h w) e").rearrange("(p i) e -> p i e", i=TILES)
         xn_dram = xn.rearrange("b h w c -> (b h w) c").rearrange("(p i) c -> p i c", i=TILES)
@@ -48,14 +46,14 @@ def tile_transformerconvblock_pb_kernel(
         wo_dram = W_O.rearrange("(q t) c -> q t c", t=PACK)
 
         bias_rows = keep.tile([P, CHUNK], BF16)
-        attn_bf16 = keep.tile([P, 1], BF16)
-        ffn_bf16 = keep.tile([P, 1], BF16)
-        attn = keep.tile([P, 1], F32)
-        ffn = keep.tile([P, 1], F32)
+        scalars = keep.tile([P, 32], BF16)
+        factors = keep.tile([P, 32], F32)
+        attn = factors[:, 0:1]
+        ffn = factors[:, 16:17]
         warm = keep.tile([P, 1], F32)
         ident_f32 = keep.tile([P, P], F32)
         ident_bf16 = keep.tile([P, P], BF16)
-        zeros = keep.tile([P, CHUNK], BF16)
+        zeros = keep.tile([P, P], BF16)
         wo_raw = keep.tile([P, PACK * K], BF16)
         o_sb = keep.tile([P, TILES * K], BF16)
         xn_sb = keep.tile([P, TILES * K], BF16)
@@ -100,13 +98,13 @@ def tile_transformerconvblock_pb_kernel(
 
         def fill(bank):
             nc.tensor.matmul(
-                out=bank[:].rearrange("q a u p -> q (a u p)"), lhsT=zeros[:, :P], rhs=zeros[:], start=True, stop=True
+                out=bank[:].rearrange("q a u p -> q (a u p)"), lhsT=zeros[:], rhs=zeros[:, 0:1].to_broadcast([P, CHUNK]), start=True, stop=True
             )
 
         def transpose_tokens(words, grouped_words, pair):
             i = 2 * pair
-            bank = psum_words.tile([P, 2, 2, P], F32, name="bank", tag="words")
-            if pair == 1:
+            bank = psum.tile([P, 2, 2, P], F32, name="bank", tag="bank")
+            if words is o_words and pair == 1:
                 fill(bank)
             for a in range(2):
                 for u in range(2):
@@ -124,8 +122,8 @@ def tile_transformerconvblock_pb_kernel(
 
         def transpose_w(k):
             n, r = k // 2, 2 * (k % 2)
-            bank = psum_words.tile([P, 2, 2, P], F32, name="bank", tag="words")
-            if k in (0, 1, 2, 4, 5):
+            bank = psum.tile([P, 2, 2, P], F32, name="bank", tag="bank")
+            if k in (1, 2, 4):
                 fill(bank)
             for a in range(2):
                 for u in range(2):
@@ -137,7 +135,7 @@ def tile_transformerconvblock_pb_kernel(
 
         def spread_bias(half, copy):
             b = half * 2 * CHUNK
-            bank = psum_u.tile([P, 2 * CHUNK], BF16, name="bias_bank", tag="u")
+            bank = psum.tile([P, 2 * CHUNK], BF16, name="bias_bank", tag="bank")
             for c in range(2):
                 n = 2 * half + c
                 nc.tensor.matmul(
@@ -152,14 +150,21 @@ def tile_transformerconvblock_pb_kernel(
         p_banks = {}
         u_banks = {}
 
+        def spread_factors():
+            bank = psum.tile([P, 32], F32, name="factor_bank", tag="bank")
+            nc.tensor.matmul(
+                out=bank[:], lhsT=ident_bf16[:, 0:1].to_broadcast([P, P]), rhs=scalars[:], start=True, stop=True
+            )
+            nc.scalar.copy(out=factors[:], in_=bank[:])
+
         def warm_up(count):
-            bank = psum_u.tile([P, CHUNK], F32, name="idle_bank", tag="u")
+            bank = psum.tile([P, CHUNK], F32, name="idle_bank", tag="bank")
             for c in range(count):
-                nc.tensor.matmul(out=bank[:], lhsT=zeros[:, :P], rhs=zeros[:], start=True, stop=True)
+                nc.tensor.matmul(out=bank[:], lhsT=zeros[:], rhs=zeros[:, 0:1].to_broadcast([P, CHUNK]), start=True, stop=True)
 
         def first_matmul(i):
             tokens = slice(i * P, (i + 1) * P)
-            p_banks[i] = psum_first.tile([P, PACK, P], F32, name="p_bank", tag="first")
+            p_banks[i] = psum.tile([P, PACK, P], F32, name="p_bank", tag="bank")
             for t in range(PACK):
                 channels = slice(t * P, (t + 1) * P)
                 nc.tensor.matmul_mx(
@@ -177,7 +182,7 @@ def tile_transformerconvblock_pb_kernel(
             nc.vector.scalar_tensor_tensor(
                 out=y_grouped[:, cols].rearrange("q (p t) -> q p t", t=PACK),
                 in0=p_banks[i][:].rearrange("q t p -> q p t"),
-                scalar=attn[:, 0:1],
+                scalar=attn,
                 in1=xn_grouped[:, cols].rearrange("q (p t) -> q p t", t=PACK),
                 op0=ALU.mult,
                 op1=ALU.add,
@@ -197,7 +202,7 @@ def tile_transformerconvblock_pb_kernel(
             j, n = tile_and_chunk(b)
             tokens = slice(j * P, (j + 1) * P)
             cols = slice(n * CHUNK, (n + 1) * CHUNK)
-            u_banks[b] = psum_u.tile([P, CHUNK], F32, name="u_bank", tag="u")
+            u_banks[b] = psum.tile([P, CHUNK], F32, name="u_bank", tag="bank")
             nc.tensor.matmul_mx(
                 out=u_banks[b][:],
                 lhsT=y_codes[:, tokens].bitcast(FP8X4),
@@ -230,7 +235,7 @@ def tile_transformerconvblock_pb_kernel(
             for c in range(0, 2 * CHUNK, width):
                 part = h[:, c : c + width]
                 first = n * CHUNK + c
-                nc.scalar.activation(out=part, in_=part, func=ACT.Relu, scale=ffn[:, 0:1])
+                nc.scalar.activation(out=part, in_=part, func=ACT.Relu, scale=ffn)
                 nc.sync.dma_start(out=out_dram[:, j, first : first + width], in_=part)
 
         def quantise_o(pair):
@@ -248,15 +253,15 @@ def tile_transformerconvblock_pb_kernel(
 
         def load_everything():
             nc.vector.memset(zeros[:], 0.0)
+            nc.vector.memset(scalars[:], 0.0)
             nc.vector.memset(bias_rows[:], 0.0)
             load(o_tiles, o_dram, 0, 2)
             nc.sync.dma_start(out=wo_raw[:].rearrange("q (t c) -> q t c", t=PACK), in_=wo_dram)
             nc.sync.dma_start(out=bias_rows[0:CHUNKS, :], in_=ffn1_b.rearrange("(n f) -> n f", n=CHUNKS))
+            nc.sync.dma_start(out=scalars[0:1, 0:1], in_=scale_attn.rearrange("(a b) -> a b", a=1))
+            nc.sync.dma_start(out=scalars[0:1, 16:17], in_=scale_ffn.rearrange("(a b) -> a b", a=1))
             load(xn_tiles, xn_dram, 0, 2)
             nc.sync.dma_start(out=w_chunks[:, 0], in_=w_dram[:, 0])
-            with nc.allow_non_contiguous_dma(reason="one bfloat16 scalar to every partition"):
-                nc.sync.dma_start(out=attn_bf16[:], in_=scale_attn.partition_broadcast(P))
-                nc.sync.dma_start(out=ffn_bf16[:], in_=scale_ffn.partition_broadcast(P))
             nc.sync.dma_start(out=w_chunks[:, 1], in_=w_dram[:, 1])
             load(o_tiles, o_dram, 2, TILES)
             load(xn_tiles, xn_dram, 2, TILES)
@@ -269,8 +274,6 @@ def tile_transformerconvblock_pb_kernel(
             nc.vector.memset(warm[:], 0.0)
             nc.scalar.activation(out=warm[:], in_=warm[:], func=ACT.Relu)
             nc.vector.tensor_copy(out=ident_bf16[:], in_=ident_f32[:])
-            nc.gpsimd.tensor_copy(out=attn[:], in_=attn_bf16[:])
-            nc.gpsimd.tensor_copy(out=ffn[:], in_=ffn_bf16[:])
 
         wo_to = wo_grouped[:].rearrange("q (t m r) -> q t m r", t=PACK, r=PACK)
         wo_from = wo_raw[:].rearrange("q (r m t) -> q t m r", t=PACK, r=PACK)
@@ -279,77 +282,71 @@ def tile_transformerconvblock_pb_kernel(
         load_everything()
         make_constants()
 
-        warm_up(3)
+        warm_up(4)
         transpose_o(0)
+        warm_up(2)
         nc.vector.tensor_copy(out=wo_to[:, :, :WO_SPLIT, :], in_=wo_from[:, :, :WO_SPLIT, :])
         nc.scalar.copy(out=wo_to[:, :, WO_SPLIT:, :], in_=wo_from[:, :, WO_SPLIT:, :])
         quantise_o(0)
         quantise(wo_grouped, wo_codes, wo_scales, 0, K)
         spread_bias(0, nc.vector.tensor_copy)
+        spread_factors()
+        spread_bias(1, nc.scalar.copy)
         transpose_xn(0)
         transpose_w(0)
         first_matmul(0)
         transpose_w(1)
         first_matmul(1)
         add_xn(0)
-        relu_y(0)
-        quantise_y(0)
         transpose_w(2)
         transpose_w(3)
+        relu_y(0)
+        quantise_y(0)
         quantise_w(0)
+        add_xn(1)
         second_matmul(0)
         transpose_o(1)
         transpose_xn(1)
-        add_xn(1)
-        quantise_w(1)
         relu_y(1)
+        quantise_w(1)
+        quantise_y(1)
         second_matmul(1)
+        second_matmul(2)
 
+        chain_start = {1: -1, 2: 8, 3: 12}
+        w_banks_at = {1: (4,), 2: (5,), 3: (6, 7)}
+        issued = 2
         for s in range(BANKS + LAG):
-            if s in (0, 1, 3, 4):
-                transpose_w(s + 4 if s < 2 else s + 3)
-            if s == 2:
-                spread_bias(1, nc.scalar.copy)
-            if s in (6, 9):
-                transpose_o(s // 3)
-            if s in (7, 10):
-                transpose_xn(s // 3)
             if s < BANKS:
                 add_bias(s)
-            if s >= LAG and (s - LAG) % 2 == 0:
+            if s >= LAG and (s - LAG) % 2 == 0 and (s - LAG) // 2 < BANKS // 2:
                 relu_h((s - LAG) // 2)
-            if s == 0:
-                quantise_y(1)
-                quantise_o(1)
-                first_matmul(2)
-                first_matmul(3)
-            if s == 1:
-                add_xn(2)
-            if s == 2:
-                relu_y(2)
-                quantise_y(2)
-                add_xn(3)
-            if s == 3:
-                relu_y(3)
-            if s == 4:
-                quantise_y(3)
-            if s in (4, 6):
-                quantise_w(s // 2)
-            for pair, first in ((2, 8), (3, 13)):
+            for pair, first in chain_start.items():
                 a = 2 * pair
-                if s == first:
+                if s == max(first, 0):
                     quantise_o(pair)
+                if s == first + 1:
                     first_matmul(a)
                     first_matmul(a + 1)
                 if s == first + 2:
                     add_xn(a)
                 if s == first + 3:
                     add_xn(a + 1)
-                if s == first + 4:
                     relu_y(a)
+                if s == first + 4:
+                    quantise_y(a)
                     relu_y(a + 1)
                 if s == first + 5:
-                    quantise_y(a)
                     quantise_y(a + 1)
-            if s + AHEAD < BANKS:
-                second_matmul(s + AHEAD)
+            if s in (3, 6):
+                quantise_w(s // 3 + 1)
+            for k in w_banks_at.get(s, ()):
+                transpose_w(k)
+            if s in (5, 7):
+                transpose_o(s // 2)
+            if s in (6, 9):
+                transpose_xn(s // 3)
+            last = 3 if s < 3 else 5 if s == 3 else s + AHEAD
+            while issued < min(last, BANKS - 1):
+                issued += 1
+                second_matmul(issued)

@@ -23,7 +23,8 @@ ROWS = CHUNK // P
 PAIRS = TILES // 2
 ROUND = 4 * CHUNKS
 BANKS = PAIRS // 2 * ROUND
-LAG = 4
+LAG = 3
+LAST_PIECES = 2
 AHEAD = 3
 WO_SPLIT = 104
 
@@ -123,7 +124,7 @@ def tile_transformerconvblock_pb_kernel(
         def transpose_w(k):
             n, r = k // 2, 2 * (k % 2)
             bank = psum.tile([P, 2, 2, P], F32, name="bank", tag="bank")
-            if k in (1, 2, 4):
+            if k in (2, 3, 5):
                 fill(bank)
             for a in range(2):
                 for u in range(2):
@@ -217,26 +218,28 @@ def tile_transformerconvblock_pb_kernel(
 
         def add_bias(b):
             j, n = tile_and_chunk(b)
-            cols = slice(n * CHUNK, (n + 1) * CHUNK)
             if b % 2 == 0:
                 h_tiles[b // 2] = results.tile([P, 2 * CHUNK], F32, name="h_tile", tag="h")
-            nc.vector.tensor_tensor(
-                out=h_tiles[b // 2][:, b % 2 * CHUNK : (b % 2 + 1) * CHUNK],
-                in0=u_banks[b][:],
-                in1=bias_all[:, cols],
-                op=ALU.add,
-            )
+            width = CHUNK // LAST_PIECES if b == BANKS - 1 else CHUNK
+            for c in range(0, CHUNK, width):
+                nc.vector.tensor_tensor(
+                    out=h_tiles[b // 2][:, b % 2 * CHUNK + c : b % 2 * CHUNK + c + width],
+                    in0=u_banks[b][:, c : c + width],
+                    in1=bias_all[:, n * CHUNK + c : n * CHUNK + c + width],
+                    op=ALU.add,
+                )
 
         def relu_h(d):
             j, n = tile_and_chunk(2 * d)
             h = h_tiles[d][:]
-            pieces = 2 if d == BANKS // 2 - 1 else 1
-            width = 2 * CHUNK // pieces
-            for c in range(0, 2 * CHUNK, width):
+            pieces = (CHUNK,) + (CHUNK // LAST_PIECES,) * LAST_PIECES if d == BANKS // 2 - 1 else (2 * CHUNK,)
+            c = 0
+            for width in pieces:
                 part = h[:, c : c + width]
                 first = n * CHUNK + c
                 nc.scalar.activation(out=part, in_=part, func=ACT.Relu, scale=ffn)
                 nc.sync.dma_start(out=out_dram[:, j, first : first + width], in_=part)
+                c += width
 
         def quantise_o(pair):
             quantise(o_grouped, o_codes, o_scales, 2 * pair * P, 2 * P)
@@ -295,26 +298,25 @@ def tile_transformerconvblock_pb_kernel(
         transpose_xn(0)
         transpose_w(0)
         first_matmul(0)
-        transpose_w(1)
         first_matmul(1)
+        transpose_w(1)
         add_xn(0)
         transpose_w(2)
         transpose_w(3)
+        add_xn(1)
         relu_y(0)
+        relu_y(1)
         quantise_y(0)
         quantise_w(0)
-        add_xn(1)
-        second_matmul(0)
         transpose_o(1)
+        second_matmul(0)
         transpose_xn(1)
-        relu_y(1)
-        quantise_w(1)
         quantise_y(1)
+        quantise_w(1)
         second_matmul(1)
         second_matmul(2)
 
-        chain_start = {1: -1, 2: 8, 3: 12}
-        w_banks_at = {1: (4,), 2: (5,), 3: (6, 7)}
+        chain_start = {1: -1, 2: 9, 3: 13}
         issued = 2
         for s in range(BANKS + LAG):
             if s < BANKS:
@@ -338,14 +340,14 @@ def tile_transformerconvblock_pb_kernel(
                     relu_y(a + 1)
                 if s == first + 5:
                     quantise_y(a + 1)
-            if s in (3, 6):
-                quantise_w(s // 3 + 1)
-            for k in w_banks_at.get(s, ()):
-                transpose_w(k)
-            if s in (5, 7):
-                transpose_o(s // 2)
-            if s in (6, 9):
-                transpose_xn(s // 3)
+            if s in (4, 6):
+                quantise_w(s // 2)
+            if 1 <= s <= 4:
+                transpose_w(s + 3)
+            if s in (6, 10):
+                transpose_o(s // 4 + 1)
+            if s in (8, 12):
+                transpose_xn(s // 4)
             last = 3 if s < 3 else 5 if s == 3 else s + AHEAD
             while issued < min(last, BANKS - 1):
                 issued += 1

@@ -26,7 +26,7 @@ BANKS = PAIRS // 2 * ROUND
 LAG = 3
 LAST_PIECES = 2
 AHEAD = 3
-WO_SPLIT = 104
+WO_SPLIT = 52
 
 FLOPS = 2 * TOKENS * K * K + 2 * TOKENS * K * F
 
@@ -278,8 +278,8 @@ def tile_transformerconvblock_pb_kernel(
             nc.scalar.activation(out=warm[:], in_=warm[:], func=ACT.Relu)
             nc.vector.tensor_copy(out=ident_bf16[:], in_=ident_f32[:])
 
-        wo_to = wo_grouped[:].rearrange("q (t m r) -> q t m r", t=PACK, r=PACK)
-        wo_from = wo_raw[:].rearrange("q (r m t) -> q t m r", t=PACK, r=PACK)
+        wo_to = wo_grouped[:].rearrange("q (t a b r) -> q a t b r", t=PACK, b=2, r=PACK)
+        wo_from = wo_raw[:].rearrange("q (r a b t) -> q a t b r", t=PACK, b=2, r=PACK)
 
         ctx.enter_context(tc.manual_schedule())
         load_everything()
@@ -288,8 +288,8 @@ def tile_transformerconvblock_pb_kernel(
         warm_up(4)
         transpose_o(0)
         warm_up(2)
-        nc.vector.tensor_copy(out=wo_to[:, :, :WO_SPLIT, :], in_=wo_from[:, :, :WO_SPLIT, :])
-        nc.scalar.copy(out=wo_to[:, :, WO_SPLIT:, :], in_=wo_from[:, :, WO_SPLIT:, :])
+        nc.vector.tensor_copy(out=wo_to[:, :WO_SPLIT], in_=wo_from[:, :WO_SPLIT])
+        nc.scalar.copy(out=wo_to[:, WO_SPLIT:], in_=wo_from[:, WO_SPLIT:])
         quantise_o(0)
         quantise(wo_grouped, wo_codes, wo_scales, 0, K)
         spread_bias(0, nc.vector.tensor_copy)

@@ -24,6 +24,9 @@ PAIRS = TILES // 2
 ROUND = 4 * CHUNKS
 BANKS = PAIRS // 2 * ROUND
 LAG = 3
+STORES = BANKS // 2
+SINGLE_RELUS = 16
+SINGLE_STORES = 3
 LAST_PIECES = 2
 AHEAD = 3
 WO_SPLIT = 52
@@ -134,19 +137,23 @@ def tile_transformerconvblock_pb_kernel(
                 in_=bank[:].rearrange("q a u j -> q j a u"),
             )
 
-        def spread_bias(half, copy):
-            b = half * 2 * CHUNK
-            bank = psum.tile([P, 2 * CHUNK], BF16, name="bias_bank", tag="bank")
+        bias_banks = {}
+
+        def spread_bias(half):
+            bias_banks[half] = psum.tile([P, 2 * CHUNK], BF16, name="bias_bank", tag="bank")
             for c in range(2):
                 n = 2 * half + c
                 nc.tensor.matmul(
-                    out=bank[:, c * CHUNK : (c + 1) * CHUNK],
+                    out=bias_banks[half][:, c * CHUNK : (c + 1) * CHUNK],
                     lhsT=ident_bf16[:, n : n + 1].to_broadcast([P, P]),
                     rhs=bias_rows[:],
                     start=True,
                     stop=True,
                 )
-            copy(out=bias_all[:, b : b + 2 * CHUNK], in_=bank[:])
+
+        def keep_bias(half, copy):
+            b = half * 2 * CHUNK
+            copy(out=bias_all[:, b : b + 2 * CHUNK], in_=bias_banks[half][:])
 
         p_banks = {}
         u_banks = {}
@@ -231,15 +238,35 @@ def tile_transformerconvblock_pb_kernel(
 
         def relu_h(d):
             j, n = tile_and_chunk(2 * d)
-            h = h_tiles[d][:]
-            pieces = (CHUNK,) + (CHUNK // LAST_PIECES,) * LAST_PIECES if d == BANKS // 2 - 1 else (2 * CHUNK,)
-            c = 0
-            for width in pieces:
+            h = h_tiles[d]
+
+            def relu(c, width):
                 part = h[:, c : c + width]
-                first = n * CHUNK + c
                 nc.scalar.activation(out=part, in_=part, func=ACT.Relu, scale=ffn)
-                nc.sync.dma_start(out=out_dram[:, j, first : first + width], in_=part)
-                c += width
+
+            def store(c, width):
+                first = n * CHUNK + c
+                nc.sync.dma_start(out=out_dram[:, j, first : first + width], in_=h[:, c : c + width])
+
+            if d < STORES - SINGLE_RELUS:
+                relu(0, 2 * CHUNK)
+                store(0, 2 * CHUNK)
+            elif d < STORES - SINGLE_STORES:
+                relu(0, CHUNK)
+                relu(CHUNK, CHUNK)
+                store(0, 2 * CHUNK)
+            elif d < STORES - 1:
+                for c in (0, CHUNK):
+                    relu(c, CHUNK)
+                    store(c, CHUNK)
+            else:
+                relu(0, CHUNK)
+                store(0, CHUNK)
+                width = CHUNK // LAST_PIECES
+                for c in range(CHUNK, 2 * CHUNK, width):
+                    part = h[:, c : c + width]
+                    nc.vector.tensor_scalar(part, part, ffn, 0.0, op0=ALU.mult, op1=ALU.max)
+                    store(c, width)
 
         def quantise_o(pair):
             quantise(o_grouped, o_codes, o_scales, 2 * pair * P, 2 * P)
@@ -292,9 +319,10 @@ def tile_transformerconvblock_pb_kernel(
         nc.scalar.copy(out=wo_to[:, WO_SPLIT:], in_=wo_from[:, WO_SPLIT:])
         quantise_o(0)
         quantise(wo_grouped, wo_codes, wo_scales, 0, K)
-        spread_bias(0, nc.vector.tensor_copy)
+        spread_bias(0)
+        keep_bias(0, nc.vector.tensor_copy)
         spread_factors()
-        spread_bias(1, nc.scalar.copy)
+        spread_bias(1)
         transpose_xn(0)
         transpose_w(0)
         first_matmul(0)
@@ -315,13 +343,14 @@ def tile_transformerconvblock_pb_kernel(
         quantise_w(1)
         second_matmul(1)
         second_matmul(2)
+        keep_bias(1, nc.scalar.copy)
 
         chain_start = {1: -1, 2: 9, 3: 13}
         issued = 2
         for s in range(BANKS + LAG):
             if s < BANKS:
                 add_bias(s)
-            if s >= LAG and (s - LAG) % 2 == 0 and (s - LAG) // 2 < BANKS // 2:
+            if s >= LAG and (s - LAG) % 2 == 0 and (s - LAG) // 2 < STORES:
                 relu_h((s - LAG) // 2)
             for pair, first in chain_start.items():
                 a = 2 * pair
@@ -333,10 +362,10 @@ def tile_transformerconvblock_pb_kernel(
                 if s == first + 2:
                     add_xn(a)
                 if s == first + 3:
-                    add_xn(a + 1)
                     relu_y(a)
-                if s == first + 4:
+                    add_xn(a + 1)
                     quantise_y(a)
+                if s == first + 4:
                     relu_y(a + 1)
                 if s == first + 5:
                     quantise_y(a + 1)
@@ -348,7 +377,7 @@ def tile_transformerconvblock_pb_kernel(
                 transpose_o(s // 4 + 1)
             if s in (8, 12):
                 transpose_xn(s // 4)
-            last = 3 if s < 3 else 5 if s == 3 else s + AHEAD
+            last = 3 if s < 2 else 5 if s < 4 else s + AHEAD
             while issued < min(last, BANKS - 1):
                 issued += 1
                 second_matmul(issued)

@@ -100,16 +100,9 @@ def tile_transformerconvblock_pb_kernel(
             "q (n j r u) -> q n j r u", n=CHUNKS, r=ROWS, u=2
         )
 
-        def fill(bank):
-            nc.tensor.matmul(
-                out=bank[:].rearrange("q a u p -> q (a u p)"), lhsT=zeros[:], rhs=zeros[:, 0:1].to_broadcast([P, CHUNK]), start=True, stop=True
-            )
-
         def transpose_tokens(words, grouped_words, pair):
             i = 2 * pair
             bank = psum.tile([P, 2, 2, P], F32, name="bank", tag="bank")
-            if words is o_words and pair == 1:
-                fill(bank)
             for a in range(2):
                 for u in range(2):
                     nc.tensor.transpose(bank[:, a, u, :], words[:, i + a, :, u], ident_f32[:])
@@ -127,8 +120,6 @@ def tile_transformerconvblock_pb_kernel(
         def transpose_w(k):
             n, r = k // 2, 2 * (k % 2)
             bank = psum.tile([P, 2, 2, P], F32, name="bank", tag="bank")
-            if k in (2, 3, 5):
-                fill(bank)
             for a in range(2):
                 for u in range(2):
                     nc.tensor.transpose(bank[:, a, u, :], w_words[:, n, r + a, :, u], ident_f32[:])
@@ -314,7 +305,6 @@ def tile_transformerconvblock_pb_kernel(
 
         warm_up(4)
         transpose_o(0)
-        warm_up(2)
         nc.vector.tensor_copy(out=wo_to[:, :WO_SPLIT], in_=wo_from[:, :WO_SPLIT])
         nc.scalar.copy(out=wo_to[:, WO_SPLIT:], in_=wo_from[:, WO_SPLIT:])
         quantise_o(0)

@@ -29,7 +29,7 @@ SINGLE_RELUS = 16
 SINGLE_STORES = 3
 LAST_PIECES = 2
 AHEAD = 3
-WO_SPLIT = 52
+WO_SPLIT = 44
 
 FLOPS = 2 * TOKENS * K * K + 2 * TOKENS * K * F
 
@@ -192,10 +192,11 @@ def tile_transformerconvblock_pb_kernel(
             nc.vector.tensor_scalar_max(y_grouped[:, cols], y_grouped[:, cols], 0.0)
 
         def tile_and_chunk(b):
-            fours, rest = divmod(b, ROUND)
-            half, rest = divmod(rest, ROUND // 2)
+            if b >= BANKS // 2:
+                return divmod(b, CHUNKS)
+            half, rest = divmod(b, BANKS // 4)
             tile, chunk = divmod(rest, 2)
-            return 4 * fours + tile, 2 * half + chunk
+            return tile, 2 * half + chunk
 
         def second_matmul(b):
             j, n = tile_and_chunk(b)
@@ -304,11 +305,11 @@ def tile_transformerconvblock_pb_kernel(
         make_constants()
 
         warm_up(4)
-        transpose_o(0)
         nc.vector.tensor_copy(out=wo_to[:, :WO_SPLIT], in_=wo_from[:, :WO_SPLIT])
         nc.scalar.copy(out=wo_to[:, WO_SPLIT:], in_=wo_from[:, WO_SPLIT:])
-        quantise_o(0)
+        transpose_o(0)
         quantise(wo_grouped, wo_codes, wo_scales, 0, K)
+        quantise_o(0)
         spread_bias(0)
         keep_bias(0, nc.vector.tensor_copy)
         spread_factors()
@@ -335,7 +336,7 @@ def tile_transformerconvblock_pb_kernel(
         second_matmul(2)
         keep_bias(1, nc.scalar.copy)
 
-        chain_start = {1: -1, 2: 9, 3: 13}
+        chain_start = {1: -1, 2: 9, 3: 16}
         issued = 2
         for s in range(BANKS + LAG):
             if s < BANKS:
@@ -363,10 +364,10 @@ def tile_transformerconvblock_pb_kernel(
                 quantise_w(s // 2)
             if 1 <= s <= 4:
                 transpose_w(s + 3)
-            if s in (6, 10):
-                transpose_o(s // 4 + 1)
-            if s in (8, 12):
-                transpose_xn(s // 4)
+            if s in (6, 12):
+                transpose_o(2 if s == 6 else 3)
+            if s in (8, 14):
+                transpose_xn(2 if s == 8 else 3)
             last = 3 if s < 2 else 5 if s < 4 else s + AHEAD
             while issued < min(last, BANKS - 1):
                 issued += 1

from contextlib import ExitStack

import concourse.masks as masks
import concourse.mybir as mybir

F32 = mybir.dt.float32
BF16 = mybir.dt.bfloat16
U32 = mybir.dt.uint32
U8 = mybir.dt.uint8
FP8X4 = mybir.dt.float8_e4m3fn_x4
ALU = mybir.AluOpType
ACT = mybir.ActivationFunctionType

P = 128
PACK = 4
TOKENS = 4 * 16 * 16
K = 512
F = 2048
TILES = TOKENS // P
CHUNK = 512
CHUNKS = F // CHUNK
ROWS = CHUNK // P
PAIRS = TILES // 2
ROUND = 4 * CHUNKS
BANKS = PAIRS // 2 * ROUND
LAG = 3
STORES = BANKS // 2
SINGLE_RELUS = 16
SINGLE_STORES = 3
LAST_PIECES = 2
AHEAD = 3
WO_SPLIT = 44

FLOPS = 2 * TOKENS * K * K + 2 * TOKENS * K * F


def tile_transformerconvblock_pb_kernel(
    tc, o, xn, W_O, scale_attn, ffn1_w, ffn1_b, scale_ffn, out
):
    nc = tc.nc
    with ExitStack() as ctx:
        keep = ctx.enter_context(tc.tile_pool(name="keep", bufs=1))
        results = ctx.enter_context(tc.tile_pool(name="results", bufs=10))
        psum = ctx.enter_context(tc.psum_pool(name="psum", bufs=8))

        o_dram = o.rearrange("b h w e -> (b h w) e").rearrange("(p i) e -> p i e", i=TILES)
        xn_dram = xn.rearrange("b h w c -> (b h w) c").rearrange("(p i) c -> p i c", i=TILES)
        out_dram = out.rearrange("b h w f -> (b h w) f").rearrange("(p i) f -> p i f", i=TILES)
        w_dram = ffn1_w.rearrange("(n j r) c -> j n r c", n=CHUNKS, r=ROWS)
        wo_dram = W_O.rearrange("(q t) c -> q t c", t=PACK)

        bias_rows = keep.tile([P, CHUNK], BF16)
        scalars = keep.tile([P, 32], BF16)
        factors = keep.tile([P, 32], F32)
        attn = factors[:, 0:1]
        ffn = factors[:, 16:17]
        warm = keep.tile([P, 1], F32)
        ident_f32 = keep.tile([P, P], F32)
        ident_bf16 = keep.tile([P, P], BF16)
        zeros = keep.tile([P, P], BF16)
        wo_raw = keep.tile([P, PACK * K], BF16)
        o_sb = keep.tile([P, TILES * K], BF16)
        xn_sb = keep.tile([P, TILES * K], BF16)
        w_sb = keep.tile([P, CHUNKS * ROWS * K], BF16)
        o_tiles = o_sb[:].rearrange("p (i e) -> p i e", i=TILES)
        xn_tiles = xn_sb[:].rearrange("p (i c) -> p i c", i=TILES)
        w_chunks = w_sb[:].rearrange("j (n r c) -> j n r c", n=CHUNKS, r=ROWS)

        wo_grouped = keep.tile([P, K * PACK], BF16, align_bytes=64)
        wo_codes = keep.tile([P, K], U32, align_bytes=64)
        wo_scales = keep.tile([P, K], U8, align_bytes=64)
        o_grouped = keep.tile([P, TOKENS * PACK], BF16, align_bytes=64)
        o_codes = keep.tile([P, TOKENS], U32, align_bytes=64)
        o_scales = keep.tile([P, TOKENS], U8, align_bytes=64)
        w_grouped = keep.tile([P, F * PACK], BF16, align_bytes=64)
        w_codes = keep.tile([P, F], U32, align_bytes=64)
        w_scales = keep.tile([P, F], U8, align_bytes=64)
        y_grouped = keep.tile([P, TOKENS * PACK], BF16, align_bytes=64)
        y_codes = keep.tile([P, TOKENS], U32, align_bytes=64)
        y_scales = keep.tile([P, TOKENS], U8, align_bytes=64)
        xn_grouped = keep.tile([P, TOKENS * PACK], BF16, align_bytes=64)
        bias_all = keep.tile([P, F], BF16)

        def quantise(grouped, codes, scales, start, count):
            nc.vector.quantize_mx(
                out=codes[:, start : start + count].bitcast(FP8X4),
                scales=scales[:, start : start + count],
                in_=grouped[:, PACK * start : PACK * (start + count)],
            )

        token_words = "p (i q u) -> p i q u"
        o_words = o_sb[:].bitcast(F32).rearrange(token_words, i=TILES, u=2)
        xn_words = xn_sb[:].bitcast(F32).rearrange(token_words, i=TILES, u=2)
        o_grouped_words = o_grouped[:].bitcast(F32).rearrange("q (i p u) -> q i p u", i=TILES, u=2)
        xn_grouped_words = xn_grouped[:].bitcast(F32).rearrange("q (i p u) -> q i p u", i=TILES, u=2)
        w_words = w_sb[:].bitcast(F32).rearrange(
            "j (n r q u) -> j n r q u", n=CHUNKS, r=ROWS, u=2
        )
        w_grouped_words = w_grouped[:].bitcast(F32).rearrange(
            "q (n j r u) -> q n j r u", n=CHUNKS, r=ROWS, u=2
        )

        def transpose_tokens(words, grouped_words, pair):
            i = 2 * pair
            bank = psum.tile([P, 2, 2, P], F32, name="bank", tag="bank")
            for a in range(2):
                for u in range(2):
                    nc.tensor.transpose(bank[:, a, u, :], words[:, i + a, :, u], ident_f32[:])
            nc.scalar.copy(
                out=grouped_words[:, i : i + 2, :, :],
                in_=bank[:].rearrange("q a u p -> q a p u"),
            )

        def transpose_o(pair):
            transpose_tokens(o_words, o_grouped_words, pair)

        def transpose_xn(pair):
            transpose_tokens(xn_words, xn_grouped_words, pair)

        def transpose_w(k):
            n, r = k // 2, 2 * (k % 2)
            bank = psum.tile([P, 2, 2, P], F32, name="bank", tag="bank")
            for a in range(2):
                for u in range(2):
                    nc.tensor.transpose(bank[:, a, u, :], w_words[:, n, r + a, :, u], ident_f32[:])
            nc.scalar.copy(
                out=w_grouped_words[:, n, :, r : r + 2, :],
                in_=bank[:].rearrange("q a u j -> q j a u"),
            )

        bias_banks = {}

        def spread_bias(half):
            bias_banks[half] = psum.tile([P, 2 * CHUNK], BF16, name="bias_bank", tag="bank")
            for c in range(2):
                n = 2 * half + c
                nc.tensor.matmul(
                    out=bias_banks[half][:, c * CHUNK : (c + 1) * CHUNK],
                    lhsT=ident_bf16[:, n : n + 1].to_broadcast([P, P]),
                    rhs=bias_rows[:],
                    start=True,
                    stop=True,
                )

        def keep_bias(half, copy):
            b = half * 2 * CHUNK
            copy(out=bias_all[:, b : b + 2 * CHUNK], in_=bias_banks[half][:])

        p_banks = {}
        u_banks = {}

        def spread_factors():
            bank = psum.tile([P, 32], F32, name="factor_bank", tag="bank")
            nc.tensor.matmul(
                out=bank[:], lhsT=ident_bf16[:, 0:1].to_broadcast([P, P]), rhs=scalars[:], start=True, stop=True
            )
            nc.scalar.copy(out=factors[:], in_=bank[:])

        def warm_up(count):
            bank = psum.tile([P, CHUNK], F32, name="idle_bank", tag="bank")
            for c in range(count):
                nc.tensor.matmul(out=bank[:], lhsT=zeros[:], rhs=zeros[:, 0:1].to_broadcast([P, CHUNK]), start=True, stop=True)

        def first_matmul(i):
            tokens = slice(i * P, (i + 1) * P)
            p_banks[i] = psum.tile([P, PACK, P], F32, name="p_bank", tag="bank")
            for t in range(PACK):
                channels = slice(t * P, (t + 1) * P)
                nc.tensor.matmul_mx(
                    out=p_banks[i][:, t, :],
                    lhsT=wo_codes[:, channels].bitcast(FP8X4),
                    lhsT_scale=wo_scales[:, channels],
                    rhs=o_codes[:, tokens].bitcast(FP8X4),
                    rhs_scale=o_scales[:, tokens],
                    start=True,
                    stop=True,
                )

        def add_xn(i):
            cols = slice(i * K, (i + 1) * K)
            nc.vector.scalar_tensor_tensor(
                out=y_grouped[:, cols].rearrange("q (p t) -> q p t", t=PACK),
                in0=p_banks[i][:].rearrange("q t p -> q p t"),
                scalar=attn,
                in1=xn_grouped[:, cols].rearrange("q (p t) -> q p t", t=PACK),
                op0=ALU.mult,
                op1=ALU.add,
            )

        def relu_y(i):
            cols = slice(i * K, (i + 1) * K)
            nc.vector.tensor_scalar_max(y_grouped[:, cols], y_grouped[:, cols], 0.0)

        def tile_and_chunk(b):
            if b >= BANKS // 2:
                return divmod(b, CHUNKS)
            half, rest = divmod(b, BANKS // 4)
            tile, chunk = divmod(rest, 2)
            return tile, 2 * half + chunk

        def second_matmul(b):
            j, n = tile_and_chunk(b)
            tokens = slice(j * P, (j + 1) * P)
            cols = slice(n * CHUNK, (n + 1) * CHUNK)
            u_banks[b] = psum.tile([P, CHUNK], F32, name="u_bank", tag="bank")
            nc.tensor.matmul_mx(
                out=u_banks[b][:],
                lhsT=y_codes[:, tokens].bitcast(FP8X4),
                lhsT_scale=y_scales[:, tokens],
                rhs=w_codes[:, cols].bitcast(FP8X4),
                rhs_scale=w_scales[:, cols],
                start=True,
                stop=True,
            )

        h_tiles = {}

        def add_bias(b):
            j, n = tile_and_chunk(b)
            if b % 2 == 0:
                h_tiles[b // 2] = results.tile([P, 2 * CHUNK], F32, name="h_tile", tag="h")
            width = CHUNK // LAST_PIECES if b == BANKS - 1 else CHUNK
            for c in range(0, CHUNK, width):
                nc.vector.tensor_tensor(
                    out=h_tiles[b // 2][:, b % 2 * CHUNK + c : b % 2 * CHUNK + c + width],
                    in0=u_banks[b][:, c : c + width],
                    in1=bias_all[:, n * CHUNK + c : n * CHUNK + c + width],
                    op=ALU.add,
                )

        def relu_h(d):
            j, n = tile_and_chunk(2 * d)
            h = h_tiles[d]

            def relu(c, width):
                part = h[:, c : c + width]
                nc.scalar.activation(out=part, in_=part, func=ACT.Relu, scale=ffn)

            def store(c, width):
                first = n * CHUNK + c
                nc.sync.dma_start(out=out_dram[:, j, first : first + width], in_=h[:, c : c + width])

            if d < STORES - SINGLE_RELUS:
                relu(0, 2 * CHUNK)
                store(0, 2 * CHUNK)
            elif d < STORES - SINGLE_STORES:
                relu(0, CHUNK)
                relu(CHUNK, CHUNK)
                store(0, 2 * CHUNK)
            elif d < STORES - 1:
                for c in (0, CHUNK):
                    relu(c, CHUNK)
                    store(c, CHUNK)
            else:
                relu(0, CHUNK)
                store(0, CHUNK)
                width = CHUNK // LAST_PIECES
                for c in range(CHUNK, 2 * CHUNK, width):
                    part = h[:, c : c + width]
                    nc.vector.tensor_scalar(part, part, ffn, 0.0, op0=ALU.mult, op1=ALU.max)
                    store(c, width)

        def quantise_o(pair):
            quantise(o_grouped, o_codes, o_scales, 2 * pair * P, 2 * P)

        def quantise_y(i):
            quantise(y_grouped, y_codes, y_scales, i * P, P)

        def quantise_w(n):
            quantise(w_grouped, w_codes, w_scales, n * CHUNK, CHUNK)

        def load(tiles, dram, first, last):
            rows = slice(first, last)
            nc.sync.dma_start(out=tiles[:, rows, :], in_=dram[:, rows, :])

        def load_everything():
            nc.vector.memset(zeros[:], 0.0)
            nc.vector.memset(scalars[:], 0.0)
            nc.vector.memset(bias_rows[:], 0.0)
            load(o_tiles, o_dram, 0, 2)
            nc.sync.dma_start(out=wo_raw[:].rearrange("q (t c) -> q t c", t=PACK), in_=wo_dram)
            nc.sync.dma_start(out=bias_rows[0:CHUNKS, :], in_=ffn1_b.rearrange("(n f) -> n f", n=CHUNKS))
            nc.sync.dma_start(out=scalars[0:1, 0:1], in_=scale_attn.rearrange("(a b) -> a b", a=1))
            nc.sync.dma_start(out=scalars[0:1, 16:17], in_=scale_ffn.rearrange("(a b) -> a b", a=1))
            load(xn_tiles, xn_dram, 0, 2)
            nc.sync.dma_start(out=w_chunks[:, 0], in_=w_dram[:, 0])
            nc.sync.dma_start(out=w_chunks[:, 1], in_=w_dram[:, 1])
            load(o_tiles, o_dram, 2, TILES)
            load(xn_tiles, xn_dram, 2, TILES)
            nc.sync.dma_start(out=w_chunks[:, 2], in_=w_dram[:, 2])
            nc.sync.dma_start(out=w_chunks[:, 3], in_=w_dram[:, 3])

        def make_constants():
            nc.gpsimd.memset(ident_f32[:], 0.0)
            masks.make_identity(nc, ident_f32[:], nomemset=True)
            nc.vector.memset(warm[:], 0.0)
            nc.scalar.activation(out=warm[:], in_=warm[:], func=ACT.Relu)
            nc.vector.tensor_copy(out=ident_bf16[:], in_=ident_f32[:])

        wo_to = wo_grouped[:].rearrange("q (t a b r) -> q a t b r", t=PACK, b=2, r=PACK)
        wo_from = wo_raw[:].rearrange("q (r a b t) -> q a t b r", t=PACK, b=2, r=PACK)

        ctx.enter_context(tc.manual_schedule())
        load_everything()
        make_constants()

        warm_up(4)
        nc.vector.tensor_copy(out=wo_to[:, :WO_SPLIT], in_=wo_from[:, :WO_SPLIT])
        nc.scalar.copy(out=wo_to[:, WO_SPLIT:], in_=wo_from[:, WO_SPLIT:])
        transpose_o(0)
        quantise(wo_grouped, wo_codes, wo_scales, 0, K)
        quantise_o(0)
        spread_bias(0)
        keep_bias(0, nc.vector.tensor_copy)
        spread_factors()
        spread_bias(1)
        transpose_xn(0)
        transpose_w(0)
        first_matmul(0)
        first_matmul(1)
        transpose_w(1)
        add_xn(0)
        transpose_w(2)
        transpose_w(3)
        add_xn(1)
        relu_y(0)
        relu_y(1)
        quantise_y(0)
        quantise_w(0)
        transpose_o(1)
        second_matmul(0)
        transpose_xn(1)
        quantise_y(1)
        quantise_w(1)
        second_matmul(1)
        second_matmul(2)
        keep_bias(1, nc.scalar.copy)

        chain_start = {1: -1, 2: 9, 3: 16}
        issued = 2
        for s in range(BANKS + LAG):
            if s < BANKS:
                add_bias(s)
            if s >= LAG and (s - LAG) % 2 == 0 and (s - LAG) // 2 < STORES:
                relu_h((s - LAG) // 2)
            for pair, first in chain_start.items():
                a = 2 * pair
                if s == max(first, 0):
                    quantise_o(pair)
                if s == first + 1:
                    first_matmul(a)
                    first_matmul(a + 1)
                if s == first + 2:
                    add_xn(a)
                if s == first + 3:
                    relu_y(a)
                    add_xn(a + 1)
                    quantise_y(a)
                if s == first + 4:
                    relu_y(a + 1)
                if s == first + 5:
                    quantise_y(a + 1)
            if s in (4, 6):
                quantise_w(s // 2)
            if 1 <= s <= 4:
                transpose_w(s + 3)
            if s in (6, 12):
                transpose_o(2 if s == 6 else 3)
            if s in (8, 14):
                transpose_xn(2 if s == 8 else 3)
            last = 3 if s < 2 else 5 if s < 4 else s + AHEAD
            while issued < min(last, BANKS - 1):
                issued += 1
                second_matmul(issued)
